import numpy as np
import ml_dtypes


def mxq(x, axis, fmt="e4m3"):
    dtype, down = {"e4m3": (ml_dtypes.float8_e4m3fn, 7), "e5m2": (ml_dtypes.float8_e5m2, 14)}[fmt]
    v = np.moveaxis(np.asarray(x, np.float32).astype(ml_dtypes.bfloat16).astype(np.float64), axis, -1)
    blocks = v.reshape(v.shape[:-1] + (-1, 32))
    amax = np.abs(blocks).max(-1, keepdims=True)
    byte = np.maximum(np.where(amax > 0, np.frexp(amax)[1] - 1 + 127, 0) - down, 1)
    scale = np.exp2(byte - 127.0)
    codes = (blocks / scale).astype(np.float32).astype(dtype).astype(np.float64)
    return np.moveaxis((codes * scale).reshape(v.shape), -1, axis)


WIDE = False


def mx_kscale(k):
    if not WIDE:
        return np.ones(k)
    levels = np.array([10, -10, 5, -5, 0])
    if k % 512:
        return np.exp2(np.random.permutation(np.resize(levels, k // 32))).repeat(32)
    a = np.empty((k // 512, 16))
    for p in range(k // 512):
        a[p, :8] = np.random.permutation(np.resize(levels, 8))
        for g in range(8):
            far = levels[np.abs(levels - a[p, g]) >= 10]
            a[p, g + 8] = far[np.random.randint(len(far))]
    return np.exp2(a.ravel()).repeat(32)


BF16 = ml_dtypes.bfloat16


def bf(x):
    return np.asarray(x, np.float32).astype(BF16)


def f64(x):
    return np.asarray(x).astype(np.float64)


B, S, D, N = 4, 2048, 512, 128
EPS = 1e-6
GS = 6.0 / np.sqrt(D)
LEVELS = np.array([-1.0, -0.5, 0.0, 0.5, 1.0])
PROBS = np.array([0.23, 0.17, 0.2, 0.17, 0.23])


def setup_inputs():
    s = mx_kscale(D)
    s2 = np.concatenate([s, s])
    return {"x_real": bf(np.random.standard_normal((B, S, D)) * 1.2 + 0.5),
            "x_imag": bf(np.random.standard_normal((B, S, D)) * 0.7 + 0.1),
            "qw_re": bf(np.random.choice(LEVELS, size=(N, D), p=PROBS) / s),
            "qw_im": bf(np.random.choice(LEVELS, size=(N, D), p=PROBS) / s),
            "gamma": bf((1.0 + 0.1 * np.random.standard_normal(D + D)) * GS * s2),
            "beta": bf(0.2 * np.random.standard_normal(D + D) * GS * s2),
            "s_re": bf(0.7 + 0.05 * np.random.standard_normal(1)),
            "s_im": bf(0.9 + 0.05 * np.random.standard_normal(1))}


def reference(x_real, x_imag, qw_re, qw_im, gamma, beta, s_re, s_im):
    x_cat = np.concatenate([f64(x_real), f64(x_imag)], axis=-1)
    mu = x_cat.mean(axis=-1, keepdims=True)
    var = x_cat.var(axis=-1, keepdims=True)
    norm = (x_cat - mu) * (1.0 / np.sqrt(var + EPS)) * f64(gamma) + f64(beta)
    nr = mxq(norm[..., :D], 2, "e4m3")
    ni = mxq(norm[..., D:], 2, "e4m3")
    wr = mxq(f64(qw_re), 1, "e4m3").T
    wi = mxq(f64(qw_im), 1, "e4m3").T
    y_real = (nr @ wr) - (ni @ wi)
    y_imag = (nr @ wi) + (ni @ wr)
    return y_real * f64(s_re), y_imag * f64(s_im)

@@ -1,0 +1,225 @@
+from contextlib import ExitStack
+
+import concourse.mybir as mybir
+from concourse.masks import make_identity
+
+F32 = mybir.dt.float32
+BF16 = mybir.dt.bfloat16
+U32 = mybir.dt.uint32
+U8 = mybir.dt.uint8
+FP8X4 = mybir.dt.float8_e4m3fn_x4
+ACT = mybir.ActivationFunctionType
+ALU = mybir.AluOpType
+
+P = 128
+PACK = 4
+ROWS = 4 * 2048
+D = 512
+N_OUT = 128
+HALVES = 2
+K_BLOCKS = HALVES * PACK
+EPS = 1e-6
+
+GROUP_TILES = 4
+GROUP_ROWS = GROUP_TILES * P
+GROUPS = ROWS // GROUP_ROWS
+VECTOR_NORM_TILES = 1
+SCALAR_REGROUP_TILES = 3
+
+FLOPS = 4 * 2 * ROWS * D * N_OUT
+
+
+def tile_realimagfourvallinear_pa_t_kernel(
+    tc, x_real, x_imag, qw_re, qw_im, gamma, beta, s_re, s_im, out_0, out_1
+):
+    nc = tc.nc
+    x_views = [
+        x.flatten_outer_dims().rearrange("(g p j) k -> g p j k", p=P, j=GROUP_TILES)
+        for x in (x_real, x_imag)
+    ]
+    y_views = [
+        y.flatten_outer_dims().rearrange("(g p j) n -> g p j n", p=P, j=GROUP_TILES)
+        for y in (out_0, out_1)
+    ]
+
+    with ExitStack() as ctx:
+        const = ctx.enter_context(tc.tile_pool(name="const", bufs=1))
+        x_pool = ctx.enter_context(tc.tile_pool(name="x_pool", bufs=GROUPS))
+
+        x_tiles = []
+        for g in range(GROUPS):
+            x_sb = x_pool.tile([P, HALVES, GROUP_TILES, D], BF16)
+            for h in range(HALVES):
+                nc.sync.dma_start(out=x_sb[:, h], in_=x_views[h][g])
+            x_tiles.append(x_sb)
+
+        ident_f32 = const.tile([P, P], F32)
+        make_identity(nc, ident_f32[:])
+        minus_half = const.tile([P, GROUP_TILES], F32)
+        nc.vector.memset(minus_half[:], -0.5)
+        gain_cols = const.tile([P, HALVES], F32)
+        affine_cols = const.tile([P, 2 * K_BLOCKS], F32)
+        w_codes = const.tile([P, HALVES * 2 * N_OUT], U32, align_bytes=64)
+        w_scales = const.tile([P, HALVES * 2 * N_OUT], U8, align_bytes=64)
+
+        with tc.tile_pool(name="setup", bufs=1) as setup, tc.psum_pool(name="setup_psum", bufs=1) as setup_psum:
+            ident_bf16 = setup.tile([P, P], BF16)
+            make_identity(nc, ident_bf16[:])
+
+            s_re_bf16 = setup.tile([P, 1], BF16)
+            s_im_bf16 = setup.tile([P, 1], BF16)
+            nc.scalar.dma_start(out=s_re_bf16[:], in_=s_re.partition_broadcast(P))
+            nc.scalar.dma_start(out=s_im_bf16[:], in_=s_im.partition_broadcast(P))
+            nc.vector.tensor_copy(out=gain_cols[:, 0:1], in_=s_re_bf16[:])
+            nc.vector.tensor_copy(out=gain_cols[:, 1:2], in_=s_im_bf16[:])
+
+            for i, vec in enumerate((gamma, beta)):
+                vec_bf16 = setup.tile([P, HALVES, PACK], BF16, name="vec_bf16_%d" % i)
+                nc.scalar.dma_start(out=vec_bf16[:], in_=vec.rearrange("(h p t) -> p h t", h=HALVES, t=PACK))
+                nc.vector.tensor_copy(
+                    out=affine_cols[:, i * K_BLOCKS : (i + 1) * K_BLOCKS], in_=vec_bf16[:].rearrange("p h t -> p (h t)")
+                )
+
+            w_t = []
+            for w in (qw_re, qw_im):
+                w_sb = setup.tile([P, D], BF16, name="w_sb", bufs=2)
+                nc.scalar.dma_start(out=w_sb[:], in_=w)
+                w_ps = setup_psum.tile([P, PACK, N_OUT], BF16, name="w_ps", bufs=2)
+                for t in range(PACK):
+                    nc.tensor.transpose(w_ps[:, t, :], w_sb[:, t:D:PACK], ident_bf16[:])
+                w_t.append(w_ps[:].rearrange("p t n -> p n t"))
+            w_grouped = setup.tile([P, HALVES * 2, N_OUT, PACK], BF16, align_bytes=64)
+            nc.vector.tensor_copy(out=w_grouped[:, 0], in_=w_t[0])
+            nc.vector.tensor_copy(out=w_grouped[:, 1], in_=w_t[1])
+            nc.vector.tensor_scalar_mul(out=w_grouped[:, 2], in0=w_t[1], scalar1=-1.0)
+            nc.vector.tensor_copy(out=w_grouped[:, 3], in_=w_t[0])
+            nc.vector.quantize_mx(
+                out=w_codes[:].bitcast(FP8X4),
+                scales=w_scales[:],
+                in_=w_grouped[:].rearrange("p q n t -> p (q n t)"),
+            )
+
+        small = ctx.enter_context(tc.tile_pool(name="small", bufs=4))
+        work = ctx.enter_context(tc.tile_pool(name="work", bufs=2))
+        t_psum = ctx.enter_context(tc.psum_pool(name="t_psum", bufs=6))
+        y_psum = ctx.enter_context(tc.psum_pool(name="y_psum", bufs=2))
+
+        neg_mean, var_eps, rstd, x_hat, planes, grouped, codes, scales, y_ps = ({} for i in range(9))
+
+        def statistics(g):
+            stats = small.tile([P, GROUP_TILES, HALVES, 6], F32)
+            mean_var = small.tile([P, GROUP_TILES, 2], F32)
+            for h in range(HALVES):
+                for j in range(GROUP_TILES):
+                    nc.vector.bn_stats(out=stats[:, j, h, :], in_=x_tiles[g][:, h, j, :])
+            for j in range(GROUP_TILES):
+                nc.vector.bn_aggr(out=mean_var[:, j, :], in_=stats[:, j].rearrange("p h c -> p (h c)"))
+            neg_mean[g] = small.tile([P, GROUP_TILES], F32, name="neg_mean")
+            nc.vector.tensor_scalar_mul(out=neg_mean[g][:], in0=mean_var[:, :, 0], scalar1=-1.0)
+            var_eps[g] = small.tile([P, GROUP_TILES], F32, name="var_eps")
+            nc.vector.tensor_scalar_add(out=var_eps[g][:], in0=mean_var[:, :, 1], scalar1=EPS)
+
+        def reciprocal_std(g):
+            rstd[g] = small.tile([P, GROUP_TILES], F32, name="rstd")
+            nc.gpsimd.tensor_tensor(out=rstd[g][:], in0=var_eps[g][:], in1=minus_half[:], op=ALU.pow)
+
+        def normalise(g):
+            x_hat[g] = work.tile([P, GROUP_TILES, HALVES, D], F32, name="x_hat")
+            for j in range(GROUP_TILES):
+                engine = nc.vector if j < VECTOR_NORM_TILES else nc.gpsimd
+                engine.tensor_scalar(
+                    out=x_hat[g][:, j].rearrange("p h (t q) -> p h t q", t=PACK),
+                    in0=x_tiles[g][:, :, j, :].rearrange("p h (q t) -> p h t q", t=PACK),
+                    scalar1=neg_mean[g][:, j : j + 1], scalar2=rstd[g][:, j : j + 1], op0=ALU.add, op1=ALU.mult,
+                )
+
+        def transpose_and_affine(g, h):
+            planes[g, h] = work.tile([P, PACK, GROUP_ROWS], BF16, name="planes_%d" % h)
+            if h == 0:
+                grouped[g] = work.tile([P, HALVES, GROUP_ROWS, PACK], BF16, align_bytes=64, name="grouped")
+            for t in range(PACK):
+                b = h * PACK + t
+                x_hat_t = t_psum.tile([P, GROUP_ROWS], F32)
+                for j in range(GROUP_TILES):
+                    nc.tensor.transpose(
+                        x_hat_t[:, j * P : (j + 1) * P], x_hat[g][:, j, h, t * P : (t + 1) * P], ident_f32[:]
+                    )
+                nc.scalar.activation(
+                    out=planes[g, h][:, t, :], in_=x_hat_t[:], func=ACT.Identity,
+                    scale=affine_cols[:, b : b + 1], bias=affine_cols[:, K_BLOCKS + b : K_BLOCKS + b + 1],
+                )
+
+        def regroup(copy, g, h, first_tile, last_tile):
+            rows = slice(first_tile * P, last_tile * P)
+            copy(
+                out=grouped[g][:, h, rows, :].rearrange("p (c i) t -> p c t i", i=4),
+                in_=planes[g, h][:, :, rows].rearrange("p t (c i) -> p c t i", i=4),
+            )
+
+        def scalar_share(g):
+            return SCALAR_REGROUP_TILES if g + 3 < GROUPS else 0
+
+        def quantise(g):
+            codes[g] = work.tile([P, HALVES, GROUP_ROWS], U32, align_bytes=64, name="codes")
+            scales[g] = work.tile([P, HALVES, GROUP_ROWS], U8, align_bytes=64, name="scales")
+            nc.vector.quantize_mx(
+                out=codes[g][:].rearrange("p h r -> p (h r)").bitcast(FP8X4),
+                scales=scales[g][:].rearrange("p h r -> p (h r)"),
+                in_=grouped[g][:].rearrange("p h r t -> p (h r t)"),
+            )
+
+        def multiply(g):
+            y_ps[g] = []
+            for pair in range(GROUP_TILES // 2):
+                y_pair = y_psum.tile([P, 2, HALVES * N_OUT], F32)
+                for i in range(2):
+                    rows = slice((2 * pair + i) * P, (2 * pair + i + 1) * P)
+                    for h in range(HALVES):
+                        cols = slice(h * 2 * N_OUT, (h + 1) * 2 * N_OUT)
+                        nc.tensor.matmul_mx(
+                            out=y_pair[:, i, :],
+                            lhsT=codes[g][:, h, rows].bitcast(FP8X4),
+                            lhsT_scale=scales[g][:, h, rows],
+                            rhs=w_codes[:, cols].bitcast(FP8X4),
+                            rhs_scale=w_scales[:, cols],
+                            start=(h == 0),
+                            stop=(h == HALVES - 1),
+                        )
+                y_ps[g].append(y_pair)
+
+        def gains_and_store(g):
+            for c in range(HALVES):
+                y_sb = work.tile([P, GROUP_TILES, N_OUT], F32, name="y_sb_%d" % c)
+                for pair in range(GROUP_TILES // 2):
+                    nc.scalar.activation(
+                        out=y_sb[:, 2 * pair : 2 * pair + 2, :], in_=y_ps[g][pair][:, :, c * N_OUT : (c + 1) * N_OUT],
+                        func=ACT.Copy, scale=gain_cols[:, c : c + 1],
+                    )
+                nc.sync.dma_start(out=y_views[c][g], in_=y_sb[:])
+
+        def in_range(g):
+            return 0 <= g < GROUPS
+
+        with tc.manual_schedule():
+            for s in range(-2, GROUPS + 2):
+                if in_range(s + 2):
+                    statistics(s + 2)
+                if in_range(s - 1):
+                    regroup(nc.vector.tensor_copy, s - 1, 0, scalar_share(s - 1), GROUP_TILES)
+                    regroup(nc.vector.tensor_copy, s - 1, 1, 0, GROUP_TILES)
+                if in_range(s + 1):
+                    normalise(s + 1)
+                if in_range(s - 1):
+                    quantise(s - 1)
+                if in_range(s - 2):
+                    multiply(s - 2)
+                if in_range(s):
+                    transpose_and_affine(s, 0)
+                    if scalar_share(s) > 0:
+                        regroup(nc.scalar.copy, s, 0, 0, scalar_share(s))
+                if in_range(s - 2):
+                    gains_and_store(s - 2)
+                if in_range(s):
+                    transpose_and_affine(s, 1)
+                if in_range(s + 2):
+                    reciprocal_std(s + 2)

@@ -17,13 +17,12 @@ ROWS = 4 * 2048
 D = 512
 N_OUT = 128
 HALVES = 2
-K_BLOCKS = HALVES * PACK
+COLS = HALVES * PACK
 EPS = 1e-6
 
 GROUP_TILES = 4
 GROUP_ROWS = GROUP_TILES * P
 GROUPS = ROWS // GROUP_ROWS
-VECTOR_NORM_TILES = 1
 SCALAR_REGROUP_TILES = 3
 
 FLOPS = 4 * 2 * ROWS * D * N_OUT
@@ -43,102 +42,109 @@ def tile_realimagfourvallinear_pa_t_kernel(
     ]
 
     with ExitStack() as ctx:
+        ctx.enter_context(tc.manual_schedule())
         const = ctx.enter_context(tc.tile_pool(name="const", bufs=1))
-        x_pool = ctx.enter_context(tc.tile_pool(name="x_pool", bufs=GROUPS))
+        x_pool = ctx.enter_context(tc.tile_pool(name="x_pool", bufs=GROUPS - 2))
+        small = ctx.enter_context(tc.tile_pool(name="small", bufs=4))
+        work = ctx.enter_context(tc.tile_pool(name="work", bufs=2))
+        deep = ctx.enter_context(tc.tile_pool(name="deep", bufs=3))
+        t_psum = ctx.enter_context(tc.psum_pool(name="t_psum", bufs=6))
+        y_psum = ctx.enter_context(tc.psum_pool(name="y_psum", bufs=2))
 
-        x_tiles = []
-        for g in range(GROUPS):
-            x_sb = x_pool.tile([P, HALVES, GROUP_TILES, D], BF16)
-            for h in range(HALVES):
-                nc.sync.dma_start(out=x_sb[:, h], in_=x_views[h][g])
-            x_tiles.append(x_sb)
+        vec_bf16 = []
+        for i, vec in enumerate((gamma, beta)):
+            vec_sb = const.tile([P, HALVES, PACK], BF16, name="vec_bf16_%d" % i)
+            nc.scalar.dma_start(out=vec_sb[:], in_=vec.rearrange("(h p t) -> p h t", h=HALVES, t=PACK))
+            vec_bf16.append(vec_sb)
+        w_sb = []
+        for i, w in enumerate((qw_re, qw_im)):
+            w_raw = const.tile([P, D], BF16, name="w_raw_%d" % i)
+            nc.scalar.dma_start(out=w_raw[:], in_=w)
+            w_sb.append(w_raw)
+        s_bf16 = []
+        for i, s in enumerate((s_re, s_im)):
+            s_sb = const.tile([P, 1], BF16, name="s_bf16_%d" % i)
+            nc.scalar.dma_start(out=s_sb[:], in_=s.partition_broadcast(P))
+            s_bf16.append(s_sb)
 
-        ident_f32 = const.tile([P, P], F32)
-        make_identity(nc, ident_f32[:])
         minus_half = const.tile([P, GROUP_TILES], F32)
         nc.vector.memset(minus_half[:], -0.5)
+        ident_f32 = const.tile([P, P], F32)
+        make_identity(nc, ident_f32[:])
+        ident_bf16 = const.tile([P, P], BF16)
         gain_cols = const.tile([P, HALVES], F32)
-        affine_cols = const.tile([P, 2 * K_BLOCKS], F32)
+        affine_cols = const.tile([P, 2 * COLS], F32)
         w_codes = const.tile([P, HALVES * 2 * N_OUT], U32, align_bytes=64)
         w_scales = const.tile([P, HALVES * 2 * N_OUT], U8, align_bytes=64)
+        w_grouped = const.tile([P, HALVES * 2, N_OUT, PACK], BF16, align_bytes=64)
 
-        with tc.tile_pool(name="setup", bufs=1) as setup, tc.psum_pool(name="setup_psum", bufs=1) as setup_psum:
-            ident_bf16 = setup.tile([P, P], BF16)
-            make_identity(nc, ident_bf16[:])
+        x_tiles, mean_var, neg_mean, var_eps, rstd, x_hat, planes, grouped, codes, scales, y_ps = ({} for i in range(11))
 
-            s_re_bf16 = setup.tile([P, 1], BF16)
-            s_im_bf16 = setup.tile([P, 1], BF16)
-            nc.scalar.dma_start(out=s_re_bf16[:], in_=s_re.partition_broadcast(P))
-            nc.scalar.dma_start(out=s_im_bf16[:], in_=s_im.partition_broadcast(P))
-            nc.vector.tensor_copy(out=gain_cols[:, 0:1], in_=s_re_bf16[:])
-            nc.vector.tensor_copy(out=gain_cols[:, 1:2], in_=s_im_bf16[:])
+        def load(g):
+            x_tiles[g] = x_pool.tile([P, HALVES, GROUP_TILES, D], BF16, name="x_sb")
+            for h in range(HALVES):
+                nc.sync.dma_start(out=x_tiles[g][:, h], in_=x_views[h][g])
 
-            for i, vec in enumerate((gamma, beta)):
-                vec_bf16 = setup.tile([P, HALVES, PACK], BF16, name="vec_bf16_%d" % i)
-                nc.scalar.dma_start(out=vec_bf16[:], in_=vec.rearrange("(h p t) -> p h t", h=HALVES, t=PACK))
-                nc.vector.tensor_copy(
-                    out=affine_cols[:, i * K_BLOCKS : (i + 1) * K_BLOCKS], in_=vec_bf16[:].rearrange("p h t -> p (h t)")
+        def prepare_constants():
+            nc.scalar.copy(out=ident_bf16[:], in_=ident_f32[:])
+            for i in range(2):
+                nc.scalar.copy(
+                    out=affine_cols[:, i * COLS : (i + 1) * COLS], in_=vec_bf16[i][:].rearrange("p h t -> p (h t)")
                 )
-
             w_t = []
-            for w in (qw_re, qw_im):
-                w_sb = setup.tile([P, D], BF16, name="w_sb", bufs=2)
-                nc.scalar.dma_start(out=w_sb[:], in_=w)
-                w_ps = setup_psum.tile([P, PACK, N_OUT], BF16, name="w_ps", bufs=2)
+            for i in range(2):
+                w_ps = y_psum.tile([P, PACK, N_OUT], BF16, name="y_pair")
                 for t in range(PACK):
-                    nc.tensor.transpose(w_ps[:, t, :], w_sb[:, t:D:PACK], ident_bf16[:])
+                    nc.tensor.transpose(w_ps[:, t, :], w_sb[i][:, t:D:PACK], ident_bf16[:])
                 w_t.append(w_ps[:].rearrange("p t n -> p n t"))
-            w_grouped = setup.tile([P, HALVES * 2, N_OUT, PACK], BF16, align_bytes=64)
-            nc.vector.tensor_copy(out=w_grouped[:, 0], in_=w_t[0])
-            nc.vector.tensor_copy(out=w_grouped[:, 1], in_=w_t[1])
-            nc.vector.tensor_scalar_mul(out=w_grouped[:, 2], in0=w_t[1], scalar1=-1.0)
-            nc.vector.tensor_copy(out=w_grouped[:, 3], in_=w_t[0])
+            nc.scalar.copy(out=w_grouped[:, 0], in_=w_t[0])
+            nc.scalar.copy(out=w_grouped[:, 3], in_=w_t[0])
+            nc.scalar.copy(out=w_grouped[:, 1], in_=w_t[1])
+            nc.scalar.activation(out=w_grouped[:, 2], in_=w_t[1], func=ACT.Copy, scale=-1.0)
+            for i in range(2):
+                nc.scalar.copy(out=gain_cols[:, i : i + 1], in_=s_bf16[i][:])
+
+        def quantise_weights():
             nc.vector.quantize_mx(
                 out=w_codes[:].bitcast(FP8X4),
                 scales=w_scales[:],
                 in_=w_grouped[:].rearrange("p q n t -> p (q n t)"),
             )
 
-        small = ctx.enter_context(tc.tile_pool(name="small", bufs=4))
-        work = ctx.enter_context(tc.tile_pool(name="work", bufs=2))
-        t_psum = ctx.enter_context(tc.psum_pool(name="t_psum", bufs=6))
-        y_psum = ctx.enter_context(tc.psum_pool(name="y_psum", bufs=2))
-
-        neg_mean, var_eps, rstd, x_hat, planes, grouped, codes, scales, y_ps = ({} for i in range(9))
-
         def statistics(g):
             stats = small.tile([P, GROUP_TILES, HALVES, 6], F32)
-            mean_var = small.tile([P, GROUP_TILES, 2], F32)
+            mean_var[g] = small.tile([P, GROUP_TILES, 2], F32, name="mean_var")
             for h in range(HALVES):
                 for j in range(GROUP_TILES):
                     nc.vector.bn_stats(out=stats[:, j, h, :], in_=x_tiles[g][:, h, j, :])
             for j in range(GROUP_TILES):
-                nc.vector.bn_aggr(out=mean_var[:, j, :], in_=stats[:, j].rearrange("p h c -> p (h c)"))
-            neg_mean[g] = small.tile([P, GROUP_TILES], F32, name="neg_mean")
-            nc.vector.tensor_scalar_mul(out=neg_mean[g][:], in0=mean_var[:, :, 0], scalar1=-1.0)
+                nc.vector.bn_aggr(out=mean_var[g][:, j, :], in_=stats[:, j].rearrange("p h c -> p (h c)"))
             var_eps[g] = small.tile([P, GROUP_TILES], F32, name="var_eps")
-            nc.vector.tensor_scalar_add(out=var_eps[g][:], in0=mean_var[:, :, 1], scalar1=EPS)
+            nc.vector.tensor_scalar_add(out=var_eps[g][:], in0=mean_var[g][:, :, 1], scalar1=EPS)
 
         def reciprocal_std(g):
             rstd[g] = small.tile([P, GROUP_TILES], F32, name="rstd")
             nc.gpsimd.tensor_tensor(out=rstd[g][:], in0=var_eps[g][:], in1=minus_half[:], op=ALU.pow)
 
+        def release_normalise(g):
+            neg_mean[g] = small.tile([P, GROUP_TILES], F32, name="neg_mean")
+            nc.vector.tensor_scalar_mul(out=neg_mean[g][:], in0=mean_var[g][:, :, 0], scalar1=-1.0)
+
         def normalise(g):
             x_hat[g] = work.tile([P, GROUP_TILES, HALVES, D], F32, name="x_hat")
             for j in range(GROUP_TILES):
-                engine = nc.vector if j < VECTOR_NORM_TILES else nc.gpsimd
-                engine.tensor_scalar(
+                nc.gpsimd.tensor_scalar(
                     out=x_hat[g][:, j].rearrange("p h (t q) -> p h t q", t=PACK),
                     in0=x_tiles[g][:, :, j, :].rearrange("p h (q t) -> p h t q", t=PACK),
                     scalar1=neg_mean[g][:, j : j + 1], scalar2=rstd[g][:, j : j + 1], op0=ALU.add, op1=ALU.mult,
                 )
 
         def transpose_and_affine(g, h):
-            planes[g, h] = work.tile([P, PACK, GROUP_ROWS], BF16, name="planes_%d" % h)
+            planes[g, h] = deep.tile([P, PACK, GROUP_ROWS], BF16, name="planes_%d" % h)
             if h == 0:
-                grouped[g] = work.tile([P, HALVES, GROUP_ROWS, PACK], BF16, align_bytes=64, name="grouped")
+                grouped[g] = deep.tile([P, HALVES, GROUP_ROWS, PACK], BF16, align_bytes=64, name="grouped")
             for t in range(PACK):
-                b = h * PACK + t
+                c = h * PACK + t
                 x_hat_t = t_psum.tile([P, GROUP_ROWS], F32)
                 for j in range(GROUP_TILES):
                     nc.tensor.transpose(
@@ -146,7 +152,7 @@ def tile_realimagfourvallinear_pa_t_kernel(
                     )
                 nc.scalar.activation(
                     out=planes[g, h][:, t, :], in_=x_hat_t[:], func=ACT.Identity,
-                    scale=affine_cols[:, b : b + 1], bias=affine_cols[:, K_BLOCKS + b : K_BLOCKS + b + 1],
+                    scale=affine_cols[:, c : c + 1], bias=affine_cols[:, COLS + c : COLS + c + 1],
                 )
 
         def regroup(copy, g, h, first_tile, last_tile):
@@ -171,7 +177,7 @@ def tile_realimagfourvallinear_pa_t_kernel(
         def multiply(g):
             y_ps[g] = []
             for pair in range(GROUP_TILES // 2):
-                y_pair = y_psum.tile([P, 2, HALVES * N_OUT], F32)
+                y_pair = y_psum.tile([P, 2, HALVES * N_OUT], F32, name="y_pair")
                 for i in range(2):
                     rows = slice((2 * pair + i) * P, (2 * pair + i + 1) * P)
                     for h in range(HALVES):
@@ -200,26 +206,31 @@ def tile_realimagfourvallinear_pa_t_kernel(
         def in_range(g):
             return 0 <= g < GROUPS
 
-        with tc.manual_schedule():
-            for s in range(-2, GROUPS + 2):
-                if in_range(s + 2):
-                    statistics(s + 2)
-                if in_range(s - 1):
-                    regroup(nc.vector.tensor_copy, s - 1, 0, scalar_share(s - 1), GROUP_TILES)
-                    regroup(nc.vector.tensor_copy, s - 1, 1, 0, GROUP_TILES)
-                if in_range(s + 1):
-                    normalise(s + 1)
-                if in_range(s - 1):
-                    quantise(s - 1)
-                if in_range(s - 2):
-                    multiply(s - 2)
-                if in_range(s):
-                    transpose_and_affine(s, 0)
-                    if scalar_share(s) > 0:
-                        regroup(nc.scalar.copy, s, 0, 0, scalar_share(s))
-                if in_range(s - 2):
-                    gains_and_store(s - 2)
-                if in_range(s):
-                    transpose_and_affine(s, 1)
-                if in_range(s + 2):
-                    reciprocal_std(s + 2)
+        for g in range(GROUPS):
+            load(g)
+        statistics(0)
+        reciprocal_std(0)
+        prepare_constants()
+
+        for s in range(GROUPS + 3):
+            if in_range(s):
+                release_normalise(s)
+                normalise(s)
+            if in_range(s + 1):
+                statistics(s + 1)
+                reciprocal_std(s + 1)
+            if s == 1:
+                quantise_weights()
+            if in_range(s - 2):
+                regroup(nc.vector.tensor_copy, s - 2, 0, scalar_share(s - 2), GROUP_TILES)
+                regroup(nc.vector.tensor_copy, s - 2, 1, 0, GROUP_TILES)
+                quantise(s - 2)
+            if in_range(s - 3):
+                gains_and_store(s - 3)
+            if in_range(s):
+                transpose_and_affine(s, 0)
+                if scalar_share(s) > 0:
+                    regroup(nc.scalar.copy, s, 0, 0, scalar_share(s))
+                transpose_and_affine(s, 1)
+            if in_range(s - 2):
+                multiply(s - 2)

@@ -23,7 +23,7 @@ EPS = 1e-6
 GROUP_TILES = 4
 GROUP_ROWS = GROUP_TILES * P
 GROUPS = ROWS // GROUP_ROWS
-SCALAR_REGROUP_TILES = 3
+GPSIMD_NORM_TILES = 2
 
 FLOPS = 4 * 2 * ROWS * D * N_OUT
 
@@ -78,7 +78,9 @@ def tile_realimagfourvallinear_pa_t_kernel(
         w_scales = const.tile([P, HALVES * 2 * N_OUT], U8, align_bytes=64)
         w_grouped = const.tile([P, HALVES * 2, N_OUT, PACK], BF16, align_bytes=64)
 
-        x_tiles, mean_var, neg_mean, var_eps, rstd, x_hat, planes, grouped, codes, scales, y_ps = ({} for i in range(11))
+        x_tiles, neg_mean, released_mean, var_eps, rstd, x_hat, planes, grouped, codes, scales, y_ps = (
+            {} for i in range(11)
+        )
 
         def load(g):
             x_tiles[g] = x_pool.tile([P, HALVES, GROUP_TILES, D], BF16, name="x_sb")
@@ -113,31 +115,34 @@ def tile_realimagfourvallinear_pa_t_kernel(
 
         def statistics(g):
             stats = small.tile([P, GROUP_TILES, HALVES, 6], F32)
-            mean_var[g] = small.tile([P, GROUP_TILES, 2], F32, name="mean_var")
+            mean_var = small.tile([P, GROUP_TILES, 2], F32)
             for h in range(HALVES):
                 for j in range(GROUP_TILES):
                     nc.vector.bn_stats(out=stats[:, j, h, :], in_=x_tiles[g][:, h, j, :])
             for j in range(GROUP_TILES):
-                nc.vector.bn_aggr(out=mean_var[g][:, j, :], in_=stats[:, j].rearrange("p h c -> p (h c)"))
+                nc.vector.bn_aggr(out=mean_var[:, j, :], in_=stats[:, j].rearrange("p h c -> p (h c)"))
+            neg_mean[g] = small.tile([P, GROUP_TILES], F32, name="neg_mean")
+            nc.vector.tensor_scalar_mul(out=neg_mean[g][:], in0=mean_var[:, :, 0], scalar1=-1.0)
             var_eps[g] = small.tile([P, GROUP_TILES], F32, name="var_eps")
-            nc.vector.tensor_scalar_add(out=var_eps[g][:], in0=mean_var[g][:, :, 1], scalar1=EPS)
+            nc.vector.tensor_scalar_add(out=var_eps[g][:], in0=mean_var[:, :, 1], scalar1=EPS)
 
         def reciprocal_std(g):
             rstd[g] = small.tile([P, GROUP_TILES], F32, name="rstd")
             nc.gpsimd.tensor_tensor(out=rstd[g][:], in0=var_eps[g][:], in1=minus_half[:], op=ALU.pow)
 
         def release_normalise(g):
-            neg_mean[g] = small.tile([P, GROUP_TILES], F32, name="neg_mean")
-            nc.vector.tensor_scalar_mul(out=neg_mean[g][:], in0=mean_var[g][:, :, 0], scalar1=-1.0)
+            released_mean[g] = small.tile([P, GROUP_TILES], F32, name="released_mean")
+            nc.vector.tensor_copy(out=released_mean[g][:], in_=neg_mean[g][:])
 
-        def normalise(g):
-            x_hat[g] = work.tile([P, GROUP_TILES, HALVES, D], F32, name="x_hat")
-            for j in range(GROUP_TILES):
-                nc.gpsimd.tensor_scalar(
-                    out=x_hat[g][:, j].rearrange("p h (t q) -> p h t q", t=PACK),
-                    in0=x_tiles[g][:, :, j, :].rearrange("p h (q t) -> p h t q", t=PACK),
-                    scalar1=neg_mean[g][:, j : j + 1], scalar2=rstd[g][:, j : j + 1], op0=ALU.add, op1=ALU.mult,
-                )
+        def normalise(engine, g, j):
+            if g not in x_hat:
+                x_hat[g] = work.tile([P, GROUP_TILES, HALVES, D], F32, name="x_hat")
+            minus_mean = neg_mean if engine == nc.vector else released_mean
+            engine.tensor_scalar(
+                out=x_hat[g][:, j].rearrange("p h (t q) -> p h t q", t=PACK),
+                in0=x_tiles[g][:, :, j, :].rearrange("p h (q t) -> p h t q", t=PACK),
+                scalar1=minus_mean[g][:, j : j + 1], scalar2=rstd[g][:, j : j + 1], op0=ALU.add, op1=ALU.mult,
+            )
 
         def transpose_and_affine(g, h):
             planes[g, h] = deep.tile([P, PACK, GROUP_ROWS], BF16, name="planes_%d" % h)
@@ -155,15 +160,11 @@ def tile_realimagfourvallinear_pa_t_kernel(
                     scale=affine_cols[:, c : c + 1], bias=affine_cols[:, COLS + c : COLS + c + 1],
                 )
 
-        def regroup(copy, g, h, first_tile, last_tile):
-            rows = slice(first_tile * P, last_tile * P)
+        def regroup(copy, g, h):
             copy(
-                out=grouped[g][:, h, rows, :].rearrange("p (c i) t -> p c t i", i=4),
-                in_=planes[g, h][:, :, rows].rearrange("p t (c i) -> p c t i", i=4),
+                out=grouped[g][:, h].rearrange("p (c i) t -> p c t i", i=4),
+                in_=planes[g, h][:].rearrange("p t (c i) -> p c t i", i=4),
             )
-
-        def scalar_share(g):
-            return SCALAR_REGROUP_TILES if g + 3 < GROUPS else 0
 
         def quantise(g):
             codes[g] = work.tile([P, HALVES, GROUP_ROWS], U32, align_bytes=64, name="codes")
@@ -206,31 +207,39 @@ def tile_realimagfourvallinear_pa_t_kernel(
         def in_range(g):
             return 0 <= g < GROUPS
 
+        def normalise_on_vector(g, first, last):
+            if in_range(g):
+                for j in range(first, last):
+                    normalise(nc.vector, g, j)
+
         for g in range(GROUPS):
             load(g)
         statistics(0)
         reciprocal_std(0)
         prepare_constants()
+        normalise_on_vector(0, GPSIMD_NORM_TILES, GROUP_TILES)
 
         for s in range(GROUPS + 3):
             if in_range(s):
                 release_normalise(s)
-                normalise(s)
+                for j in range(GPSIMD_NORM_TILES):
+                    normalise(nc.gpsimd, s, j)
             if in_range(s + 1):
                 statistics(s + 1)
                 reciprocal_std(s + 1)
             if s == 1:
                 quantise_weights()
             if in_range(s - 2):
-                regroup(nc.vector.tensor_copy, s - 2, 0, scalar_share(s - 2), GROUP_TILES)
-                regroup(nc.vector.tensor_copy, s - 2, 1, 0, GROUP_TILES)
+                regroup(nc.vector.tensor_copy, s - 2, 1)
+            normalise_on_vector(s + 1, GPSIMD_NORM_TILES, GPSIMD_NORM_TILES + 1)
+            if in_range(s - 2):
                 quantise(s - 2)
+            normalise_on_vector(s + 1, GPSIMD_NORM_TILES + 1, GROUP_TILES)
             if in_range(s - 3):
                 gains_and_store(s - 3)
             if in_range(s):
                 transpose_and_affine(s, 0)
-                if scalar_share(s) > 0:
-                    regroup(nc.scalar.copy, s, 0, 0, scalar_share(s))
+                regroup(nc.scalar.copy, s, 0)
                 transpose_and_affine(s, 1)
             if in_range(s - 2):
                 multiply(s - 2)

@@ -18,12 +18,13 @@ D = 512
 N_OUT = 128
 HALVES = 2
 COLS = HALVES * PACK
+RUN = 8
 EPS = 1e-6
 
 GROUP_TILES = 4
 GROUP_ROWS = GROUP_TILES * P
 GROUPS = ROWS // GROUP_ROWS
-GPSIMD_NORM_TILES = 2
+GPSIMD_NORM_TILES = 3
 
 FLOPS = 4 * 2 * ROWS * D * N_OUT
 
@@ -44,18 +45,23 @@ def tile_realimagfourvallinear_pa_t_kernel(
     with ExitStack() as ctx:
         ctx.enter_context(tc.manual_schedule())
         const = ctx.enter_context(tc.tile_pool(name="const", bufs=1))
-        x_pool = ctx.enter_context(tc.tile_pool(name="x_pool", bufs=GROUPS - 2))
+        x_pool = ctx.enter_context(tc.tile_pool(name="x_pool", bufs=12))
         small = ctx.enter_context(tc.tile_pool(name="small", bufs=4))
         work = ctx.enter_context(tc.tile_pool(name="work", bufs=2))
         deep = ctx.enter_context(tc.tile_pool(name="deep", bufs=3))
+        deeper = ctx.enter_context(tc.tile_pool(name="deeper", bufs=4))
         t_psum = ctx.enter_context(tc.psum_pool(name="t_psum", bufs=6))
         y_psum = ctx.enter_context(tc.psum_pool(name="y_psum", bufs=2))
 
-        vec_bf16 = []
+        affine_rows = const.tile([P, P], BF16)
+        nc.vector.memset(affine_rows[:], 0.0)
         for i, vec in enumerate((gamma, beta)):
-            vec_sb = const.tile([P, HALVES, PACK], BF16, name="vec_bf16_%d" % i)
-            nc.scalar.dma_start(out=vec_sb[:], in_=vec.rearrange("(h p t) -> p h t", h=HALVES, t=PACK))
-            vec_bf16.append(vec_sb)
+            for h in range(HALVES):
+                row = i * COLS + h * PACK
+                nc.scalar.dma_start(
+                    out=affine_rows[row : row + PACK, :].rearrange("t (b q) -> t b q", q=RUN),
+                    in_=vec[h * D : (h + 1) * D].rearrange("(b t q) -> t b q", t=PACK, q=RUN),
+                )
         w_sb = []
         for i, w in enumerate((qw_re, qw_im)):
             w_raw = const.tile([P, D], BF16, name="w_raw_%d" % i)
@@ -78,27 +84,31 @@ def tile_realimagfourvallinear_pa_t_kernel(
         w_scales = const.tile([P, HALVES * 2 * N_OUT], U8, align_bytes=64)
         w_grouped = const.tile([P, HALVES * 2, N_OUT, PACK], BF16, align_bytes=64)
 
-        x_tiles, neg_mean, released_mean, var_eps, rstd, x_hat, planes, grouped, codes, scales, y_ps = (
-            {} for i in range(11)
+        x_tiles, mean_var, neg_mean, rstd, x_hat, planes, grouped, codes, scales, y_ps = (
+            {} for i in range(10)
         )
 
         def load(g):
-            x_tiles[g] = x_pool.tile([P, HALVES, GROUP_TILES, D], BF16, name="x_sb")
+            x_tiles[g] = x_pool.tile([P, GROUP_TILES, HALVES, D], BF16, name="x_sb")
             for h in range(HALVES):
-                nc.sync.dma_start(out=x_tiles[g][:, h], in_=x_views[h][g])
+                nc.sync.dma_start(out=x_tiles[g][:, :, h, :], in_=x_views[h][g])
 
         def prepare_constants():
             nc.scalar.copy(out=ident_bf16[:], in_=ident_f32[:])
-            for i in range(2):
-                nc.scalar.copy(
-                    out=affine_cols[:, i * COLS : (i + 1) * COLS], in_=vec_bf16[i][:].rearrange("p h t -> p (h t)")
-                )
+            affine_ps = y_psum.tile([P, P], BF16, name="y_pair")
+            nc.tensor.transpose(affine_ps[:], affine_rows[:], ident_bf16[:])
+            nc.scalar.copy(out=affine_cols[:], in_=affine_ps[:, 0 : 2 * COLS])
             w_t = []
+            w_ps = y_psum.tile([P, 2, PACK, N_OUT], BF16, name="y_pair")
             for i in range(2):
-                w_ps = y_psum.tile([P, PACK, N_OUT], BF16, name="y_pair")
+                w_runs = const.tile([P, PACK, P], BF16, name="w_runs_%d" % i)
+                nc.scalar.copy(
+                    out=w_runs[:].rearrange("n t (b q) -> n t b q", q=RUN),
+                    in_=w_sb[i][:].rearrange("n (b t q) -> n t b q", t=PACK, q=RUN),
+                )
                 for t in range(PACK):
-                    nc.tensor.transpose(w_ps[:, t, :], w_sb[i][:, t:D:PACK], ident_bf16[:])
-                w_t.append(w_ps[:].rearrange("p t n -> p n t"))
+                    nc.tensor.transpose(w_ps[:, i, t, :], w_runs[:, t, :], ident_bf16[:])
+                w_t.append(w_ps[:, i].rearrange("p t n -> p n t"))
             nc.scalar.copy(out=w_grouped[:, 0], in_=w_t[0])
             nc.scalar.copy(out=w_grouped[:, 3], in_=w_t[0])
             nc.scalar.copy(out=w_grouped[:, 1], in_=w_t[1])
@@ -115,45 +125,52 @@ def tile_realimagfourvallinear_pa_t_kernel(
 
         def statistics(g):
             stats = small.tile([P, GROUP_TILES, HALVES, 6], F32)
-            mean_var = small.tile([P, GROUP_TILES, 2], F32)
+            mean_var[g] = small.tile([P, GROUP_TILES, 2], F32, name="mean_var")
             for h in range(HALVES):
                 for j in range(GROUP_TILES):
-                    nc.vector.bn_stats(out=stats[:, j, h, :], in_=x_tiles[g][:, h, j, :])
+                    nc.vector.bn_stats(out=stats[:, j, h, :], in_=x_tiles[g][:, j, h, :])
             for j in range(GROUP_TILES):
-                nc.vector.bn_aggr(out=mean_var[:, j, :], in_=stats[:, j].rearrange("p h c -> p (h c)"))
-            neg_mean[g] = small.tile([P, GROUP_TILES], F32, name="neg_mean")
-            nc.vector.tensor_scalar_mul(out=neg_mean[g][:], in0=mean_var[:, :, 0], scalar1=-1.0)
-            var_eps[g] = small.tile([P, GROUP_TILES], F32, name="var_eps")
-            nc.vector.tensor_scalar_add(out=var_eps[g][:], in0=mean_var[:, :, 1], scalar1=EPS)
+                nc.vector.bn_aggr(out=mean_var[g][:, j, :], in_=stats[:, j].rearrange("p h c -> p (h c)"))
 
         def reciprocal_std(g):
+            var_eps = small.tile([P, GROUP_TILES], F32)
+            nc.gpsimd.tensor_scalar(
+                out=var_eps[:], in0=mean_var[g][:, :, 1], scalar1=1.0, scalar2=EPS, op0=ALU.mult, op1=ALU.add
+            )
             rstd[g] = small.tile([P, GROUP_TILES], F32, name="rstd")
-            nc.gpsimd.tensor_tensor(out=rstd[g][:], in0=var_eps[g][:], in1=minus_half[:], op=ALU.pow)
+            nc.gpsimd.tensor_tensor(out=rstd[g][:], in0=var_eps[:], in1=minus_half[:], op=ALU.pow)
 
         def release_normalise(g):
-            released_mean[g] = small.tile([P, GROUP_TILES], F32, name="released_mean")
-            nc.vector.tensor_copy(out=released_mean[g][:], in_=neg_mean[g][:])
+            neg_mean[g] = small.tile([P, GROUP_TILES], F32, name="neg_mean")
+            nc.vector.tensor_scalar_mul(out=neg_mean[g][:], in0=mean_var[g][:, :, 0], scalar1=-1.0)
 
-        def normalise(engine, g, j):
+        def normalise(engine, g, j, mean, op0):
             if g not in x_hat:
-                x_hat[g] = work.tile([P, GROUP_TILES, HALVES, D], F32, name="x_hat")
-            minus_mean = neg_mean if engine == nc.vector else released_mean
+                x_hat[g] = work.tile([P, GROUP_TILES, PACK, HALVES * P], F32, name="x_hat")
             engine.tensor_scalar(
-                out=x_hat[g][:, j].rearrange("p h (t q) -> p h t q", t=PACK),
-                in0=x_tiles[g][:, :, j, :].rearrange("p h (q t) -> p h t q", t=PACK),
-                scalar1=minus_mean[g][:, j : j + 1], scalar2=rstd[g][:, j : j + 1], op0=ALU.add, op1=ALU.mult,
+                out=x_hat[g][:, j].rearrange("p t (hb q) -> p t hb q", q=RUN),
+                in0=x_tiles[g][:, j].rearrange("p h k -> p (h k)").rearrange("p (hb t q) -> p t hb q", t=PACK, q=RUN),
+                scalar1=mean, scalar2=rstd[g][:, j : j + 1], op0=op0, op1=ALU.mult,
             )
+
+        def normalise_on_gpsimd(g):
+            for j in range(GPSIMD_NORM_TILES):
+                normalise(nc.gpsimd, g, j, neg_mean[g][:, j : j + 1], ALU.add)
+
+        def normalise_on_vector(g):
+            for j in range(GPSIMD_NORM_TILES, GROUP_TILES):
+                normalise(nc.vector, g, j, mean_var[g][:, j, 0:1], ALU.subtract)
 
         def transpose_and_affine(g, h):
             planes[g, h] = deep.tile([P, PACK, GROUP_ROWS], BF16, name="planes_%d" % h)
             if h == 0:
-                grouped[g] = deep.tile([P, HALVES, GROUP_ROWS, PACK], BF16, align_bytes=64, name="grouped")
+                grouped[g] = deeper.tile([P, HALVES, GROUP_ROWS, PACK], BF16, align_bytes=64, name="grouped")
             for t in range(PACK):
                 c = h * PACK + t
                 x_hat_t = t_psum.tile([P, GROUP_ROWS], F32)
                 for j in range(GROUP_TILES):
                     nc.tensor.transpose(
-                        x_hat_t[:, j * P : (j + 1) * P], x_hat[g][:, j, h, t * P : (t + 1) * P], ident_f32[:]
+                        x_hat_t[:, j * P : (j + 1) * P], x_hat[g][:, j, t, h * P : (h + 1) * P], ident_f32[:]
                     )
                 nc.scalar.activation(
                     out=planes[g, h][:, t, :], in_=x_hat_t[:], func=ACT.Identity,
@@ -207,39 +224,33 @@ def tile_realimagfourvallinear_pa_t_kernel(
         def in_range(g):
             return 0 <= g < GROUPS
 
-        def normalise_on_vector(g, first, last):
-            if in_range(g):
-                for j in range(first, last):
-                    normalise(nc.vector, g, j)
-
         for g in range(GROUPS):
             load(g)
         statistics(0)
         reciprocal_std(0)
         prepare_constants()
-        normalise_on_vector(0, GPSIMD_NORM_TILES, GROUP_TILES)
+        normalise_on_vector(0)
 
-        for s in range(GROUPS + 3):
+        for s in range(GROUPS + 4):
             if in_range(s):
                 release_normalise(s)
-                for j in range(GPSIMD_NORM_TILES):
-                    normalise(nc.gpsimd, s, j)
+                normalise_on_gpsimd(s)
             if in_range(s + 1):
                 statistics(s + 1)
                 reciprocal_std(s + 1)
             if s == 1:
                 quantise_weights()
+            if in_range(s - 3):
+                quantise(s - 3)
             if in_range(s - 2):
                 regroup(nc.vector.tensor_copy, s - 2, 1)
-            normalise_on_vector(s + 1, GPSIMD_NORM_TILES, GPSIMD_NORM_TILES + 1)
-            if in_range(s - 2):
-                quantise(s - 2)
-            normalise_on_vector(s + 1, GPSIMD_NORM_TILES + 1, GROUP_TILES)
-            if in_range(s - 3):
-                gains_and_store(s - 3)
+            if in_range(s + 1):
+                normalise_on_vector(s + 1)
+            if in_range(s - 4):
+                gains_and_store(s - 4)
             if in_range(s):
                 transpose_and_affine(s, 0)
                 regroup(nc.scalar.copy, s, 0)
                 transpose_and_affine(s, 1)
-            if in_range(s - 2):
-                multiply(s - 2)
+            if in_range(s - 3):
+                multiply(s - 3)

@@ -21,10 +21,16 @@ COLS = HALVES * PACK
 RUN = 8
 EPS = 1e-6
 
-GROUP_TILES = 4
-GROUP_ROWS = GROUP_TILES * P
-GROUPS = ROWS // GROUP_ROWS
-GPSIMD_NORM_TILES = 3
+SIZES = [4] * 16
+GROUPS = len(SIZES)
+FIRST = [sum(SIZES[:g]) * P for g in range(GROUPS)]
+XG = [3] * 16
+XS = [1] + [0] * 15
+AFFV = GROUPS - 1
+REGS = GROUPS - 1
+LR = 1
+LQ = 2
+WQ = 1
 
 FLOPS = 4 * 2 * ROWS * D * N_OUT
 
@@ -33,14 +39,8 @@ def tile_realimagfourvallinear_pa_t_kernel(
     tc, x_real, x_imag, qw_re, qw_im, gamma, beta, s_re, s_im, out_0, out_1
 ):
     nc = tc.nc
-    x_views = [
-        x.flatten_outer_dims().rearrange("(g p j) k -> g p j k", p=P, j=GROUP_TILES)
-        for x in (x_real, x_imag)
-    ]
-    y_views = [
-        y.flatten_outer_dims().rearrange("(g p j) n -> g p j n", p=P, j=GROUP_TILES)
-        for y in (out_0, out_1)
-    ]
+    def rows_of(dram, g):
+        return dram.flatten_outer_dims()[FIRST[g] : FIRST[g] + SIZES[g] * P].rearrange("(p j) k -> p j k", j=SIZES[g])
 
     with ExitStack() as ctx:
         ctx.enter_context(tc.manual_schedule())
@@ -73,8 +73,6 @@ def tile_realimagfourvallinear_pa_t_kernel(
             nc.scalar.dma_start(out=s_sb[:], in_=s.partition_broadcast(P))
             s_bf16.append(s_sb)
 
-        minus_half = const.tile([P, GROUP_TILES], F32)
-        nc.vector.memset(minus_half[:], -0.5)
         ident_f32 = const.tile([P, P], F32)
         make_identity(nc, ident_f32[:])
         ident_bf16 = const.tile([P, P], BF16)
@@ -84,22 +82,24 @@ def tile_realimagfourvallinear_pa_t_kernel(
         w_scales = const.tile([P, HALVES * 2 * N_OUT], U8, align_bytes=64)
         w_grouped = const.tile([P, HALVES * 2, N_OUT, PACK], BF16, align_bytes=64)
 
-        x_tiles, mean_var, neg_mean, rstd, x_hat, planes, grouped, codes, scales, y_ps = (
-            {} for i in range(10)
+        x_tiles, mean_var, std, neg_mean, rstd, shift, x_hat, planes, grouped, codes, scales, y_ps = (
+            {} for i in range(12)
         )
 
         def load(g):
-            x_tiles[g] = x_pool.tile([P, GROUP_TILES, HALVES, D], BF16, name="x_sb")
+            x_tiles[g] = x_pool.tile([P, SIZES[g], HALVES, D], BF16, name="x_sb")
             for h in range(HALVES):
-                nc.sync.dma_start(out=x_tiles[g][:, :, h, :], in_=x_views[h][g])
+                nc.sync.dma_start(out=x_tiles[g][:, :, h, :], in_=rows_of((x_real, x_imag)[h], g))
 
         def prepare_constants():
             nc.scalar.copy(out=ident_bf16[:], in_=ident_f32[:])
-            affine_ps = y_psum.tile([P, P], BF16, name="y_pair")
+            affine_ps = y_psum.tile([P, P], BF16, name="y_bank")
             nc.tensor.transpose(affine_ps[:], affine_rows[:], ident_bf16[:])
             nc.scalar.copy(out=affine_cols[:], in_=affine_ps[:, 0 : 2 * COLS])
+
+        def prepare_weights():
             w_t = []
-            w_ps = y_psum.tile([P, 2, PACK, N_OUT], BF16, name="y_pair")
+            w_ps = y_psum.tile([P, 2, PACK, N_OUT], BF16, name="y_bank")
             for i in range(2):
                 w_runs = const.tile([P, PACK, P], BF16, name="w_runs_%d" % i)
                 nc.scalar.copy(
@@ -124,58 +124,72 @@ def tile_realimagfourvallinear_pa_t_kernel(
             )
 
         def statistics(g):
-            stats = small.tile([P, GROUP_TILES, HALVES, 6], F32)
-            mean_var[g] = small.tile([P, GROUP_TILES, 2], F32, name="mean_var")
+            T = SIZES[g]
+            stats = small.tile([P, T, HALVES, 6], F32)
+            mean_var[g] = small.tile([P, T, 2], F32, name="mean_var")
             for h in range(HALVES):
-                for j in range(GROUP_TILES):
+                for j in range(T):
                     nc.vector.bn_stats(out=stats[:, j, h, :], in_=x_tiles[g][:, j, h, :])
-            for j in range(GROUP_TILES):
+            for j in range(T):
                 nc.vector.bn_aggr(out=mean_var[g][:, j, :], in_=stats[:, j].rearrange("p h c -> p (h c)"))
 
+        def standard_deviation(g):
+            std[g] = small.tile([P, SIZES[g]], F32, name="std")
+            nc.scalar.activation(out=std[g][:], in_=mean_var[g][:, :, 1], func=ACT.Sqrt, bias=EPS)
+
         def reciprocal_std(g):
-            var_eps = small.tile([P, GROUP_TILES], F32)
-            nc.gpsimd.tensor_scalar(
-                out=var_eps[:], in0=mean_var[g][:, :, 1], scalar1=1.0, scalar2=EPS, op0=ALU.mult, op1=ALU.add
-            )
-            rstd[g] = small.tile([P, GROUP_TILES], F32, name="rstd")
-            nc.gpsimd.tensor_tensor(out=rstd[g][:], in0=var_eps[:], in1=minus_half[:], op=ALU.pow)
+            rstd[g] = small.tile([P, SIZES[g]], F32, name="rstd")
+            nc.vector.reciprocal(out=rstd[g][:], in_=std[g][:])
 
         def release_normalise(g):
-            neg_mean[g] = small.tile([P, GROUP_TILES], F32, name="neg_mean")
+            neg_mean[g] = small.tile([P, SIZES[g]], F32, name="neg_mean")
             nc.vector.tensor_scalar_mul(out=neg_mean[g][:], in0=mean_var[g][:, :, 0], scalar1=-1.0)
 
-        def normalise(engine, g, j, mean, op0):
+        def normalise(g, kind):
+            T = SIZES[g]
             if g not in x_hat:
-                x_hat[g] = work.tile([P, GROUP_TILES, PACK, HALVES * P], F32, name="x_hat")
-            engine.tensor_scalar(
-                out=x_hat[g][:, j].rearrange("p t (hb q) -> p t hb q", q=RUN),
-                in0=x_tiles[g][:, j].rearrange("p h k -> p (h k)").rearrange("p (hb t q) -> p t hb q", t=PACK, q=RUN),
-                scalar1=mean, scalar2=rstd[g][:, j : j + 1], op0=op0, op1=ALU.mult,
+                x_hat[g] = work.tile([P, T, PACK, HALVES * P], F32, name="x_hat")
+            a, b = XG[g], XG[g] + XS[g]
+            tiles = {"G": range(a), "S": range(a, b), "V": range(b, T)}[kind]
+            for j in tiles:
+                out = x_hat[g][:, j].rearrange("p t (hb q) -> p t hb q", q=RUN)
+                x = x_tiles[g][:, j].rearrange("p h k -> p (h k)").rearrange("p (hb t q) -> p t hb q", t=PACK, q=RUN)
+                r = rstd[g][:, j : j + 1]
+                if kind == "G":
+                    nc.gpsimd.tensor_scalar(out=out, in0=x, scalar1=neg_mean[g][:, j : j + 1], scalar2=r, op0=ALU.add, op1=ALU.mult)
+                elif kind == "V":
+                    nc.vector.tensor_scalar(out=out, in0=x, scalar1=mean_var[g][:, j, 0:1], scalar2=r, op0=ALU.subtract, op1=ALU.mult)
+                else:
+                    nc.scalar.activation(out=out, in_=x, func=ACT.Identity, scale=r, bias=shift[g][:, j : j + 1])
+
+        def make_shift(g):
+            shift[g] = small.tile([P, SIZES[g]], F32, name="shift")
+            nc.vector.scalar_tensor_tensor(
+                out=shift[g][:], in0=mean_var[g][:, :, 0], scalar=-1.0, in1=rstd[g][:], op0=ALU.mult, op1=ALU.mult
             )
 
-        def normalise_on_gpsimd(g):
-            for j in range(GPSIMD_NORM_TILES):
-                normalise(nc.gpsimd, g, j, neg_mean[g][:, j : j + 1], ALU.add)
-
-        def normalise_on_vector(g):
-            for j in range(GPSIMD_NORM_TILES, GROUP_TILES):
-                normalise(nc.vector, g, j, mean_var[g][:, j, 0:1], ALU.subtract)
-
-        def transpose_and_affine(g, h):
-            planes[g, h] = deep.tile([P, PACK, GROUP_ROWS], BF16, name="planes_%d" % h)
+        def transpose_and_affine(g, h, engine):
+            T = SIZES[g]
+            planes[g, h] = deep.tile([P, PACK, T * P], BF16, name="planes_%d" % h)
             if h == 0:
-                grouped[g] = deeper.tile([P, HALVES, GROUP_ROWS, PACK], BF16, align_bytes=64, name="grouped")
+                grouped[g] = deeper.tile([P, HALVES, T * P, PACK], BF16, align_bytes=64, name="grouped")
             for t in range(PACK):
                 c = h * PACK + t
-                x_hat_t = t_psum.tile([P, GROUP_ROWS], F32)
-                for j in range(GROUP_TILES):
+                x_hat_t = t_psum.tile([P, T * P], F32)
+                for j in range(T):
                     nc.tensor.transpose(
                         x_hat_t[:, j * P : (j + 1) * P], x_hat[g][:, j, t, h * P : (h + 1) * P], ident_f32[:]
                     )
-                nc.scalar.activation(
-                    out=planes[g, h][:, t, :], in_=x_hat_t[:], func=ACT.Identity,
-                    scale=affine_cols[:, c : c + 1], bias=affine_cols[:, COLS + c : COLS + c + 1],
-                )
+                if engine == "S":
+                    nc.scalar.activation(
+                        out=planes[g, h][:, t, :], in_=x_hat_t[:], func=ACT.Identity,
+                        scale=affine_cols[:, c : c + 1], bias=affine_cols[:, COLS + c : COLS + c + 1],
+                    )
+                else:
+                    nc.vector.tensor_scalar(
+                        out=planes[g, h][:, t, :], in0=x_hat_t[:], scalar1=affine_cols[:, c : c + 1],
+                        scalar2=affine_cols[:, COLS + c : COLS + c + 1], op0=ALU.mult, op1=ALU.add,
+                    )
 
         def regroup(copy, g, h):
             copy(
@@ -184,8 +198,8 @@ def tile_realimagfourvallinear_pa_t_kernel(
             )
 
         def quantise(g):
-            codes[g] = work.tile([P, HALVES, GROUP_ROWS], U32, align_bytes=64, name="codes")
-            scales[g] = work.tile([P, HALVES, GROUP_ROWS], U8, align_bytes=64, name="scales")
+            codes[g] = work.tile([P, HALVES, SIZES[g] * P], U32, align_bytes=64, name="codes")
+            scales[g] = work.tile([P, HALVES, SIZES[g] * P], U8, align_bytes=64, name="scales")
             nc.vector.quantize_mx(
                 out=codes[g][:].rearrange("p h r -> p (h r)").bitcast(FP8X4),
                 scales=scales[g][:].rearrange("p h r -> p (h r)"),
@@ -194,14 +208,14 @@ def tile_realimagfourvallinear_pa_t_kernel(
 
         def multiply(g):
             y_ps[g] = []
-            for pair in range(GROUP_TILES // 2):
-                y_pair = y_psum.tile([P, 2, HALVES * N_OUT], F32, name="y_pair")
-                for i in range(2):
-                    rows = slice((2 * pair + i) * P, (2 * pair + i + 1) * P)
+            for c in range(HALVES):
+                y_bank = y_psum.tile([P, SIZES[g], N_OUT], F32, name="y_bank")
+                for j in range(SIZES[g]):
+                    rows = slice(j * P, (j + 1) * P)
                     for h in range(HALVES):
-                        cols = slice(h * 2 * N_OUT, (h + 1) * 2 * N_OUT)
+                        cols = slice((2 * h + c) * N_OUT, (2 * h + c + 1) * N_OUT)
                         nc.tensor.matmul_mx(
-                            out=y_pair[:, i, :],
+                            out=y_bank[:, j, :],
                             lhsT=codes[g][:, h, rows].bitcast(FP8X4),
                             lhsT_scale=scales[g][:, h, rows],
                             rhs=w_codes[:, cols].bitcast(FP8X4),
@@ -209,17 +223,13 @@ def tile_realimagfourvallinear_pa_t_kernel(
                             start=(h == 0),
                             stop=(h == HALVES - 1),
                         )
-                y_ps[g].append(y_pair)
+                y_ps[g].append(y_bank)
 
         def gains_and_store(g):
             for c in range(HALVES):
-                y_sb = work.tile([P, GROUP_TILES, N_OUT], F32, name="y_sb_%d" % c)
-                for pair in range(GROUP_TILES // 2):
-                    nc.scalar.activation(
-                        out=y_sb[:, 2 * pair : 2 * pair + 2, :], in_=y_ps[g][pair][:, :, c * N_OUT : (c + 1) * N_OUT],
-                        func=ACT.Copy, scale=gain_cols[:, c : c + 1],
-                    )
-                nc.sync.dma_start(out=y_views[c][g], in_=y_sb[:])
+                y_sb = work.tile([P, SIZES[g], N_OUT], F32, name="y_sb_%d" % c)
+                nc.scalar.activation(out=y_sb[:], in_=y_ps[g][c][:], func=ACT.Copy, scale=gain_cols[:, c : c + 1])
+                nc.sync.dma_start(out=rows_of((out_0, out_1)[c], g), in_=y_sb[:])
 
         def in_range(g):
             return 0 <= g < GROUPS
@@ -227,30 +237,45 @@ def tile_realimagfourvallinear_pa_t_kernel(
         for g in range(GROUPS):
             load(g)
         statistics(0)
-        reciprocal_std(0)
         prepare_constants()
-        normalise_on_vector(0)
+        standard_deviation(0)
+        reciprocal_std(0)
+        if XS[0]:
+            make_shift(0)
+        normalise(0, "S")
+        normalise(0, "V")
 
-        for s in range(GROUPS + 4):
+        for s in range(GROUPS + LQ + 1):
             if in_range(s):
                 release_normalise(s)
-                normalise_on_gpsimd(s)
+                normalise(s, "G")
             if in_range(s + 1):
                 statistics(s + 1)
-                reciprocal_std(s + 1)
-            if s == 1:
+            if s == WQ:
                 quantise_weights()
-            if in_range(s - 3):
-                quantise(s - 3)
-            if in_range(s - 2):
-                regroup(nc.vector.tensor_copy, s - 2, 1)
-            if in_range(s + 1):
-                normalise_on_vector(s + 1)
-            if in_range(s - 4):
-                gains_and_store(s - 4)
+            if in_range(s - LQ):
+                quantise(s - LQ)
+            if in_range(s - LR):
+                if s - LR >= REGS:
+                    regroup(nc.vector.tensor_copy, s - LR, 0)
+                regroup(nc.vector.tensor_copy, s - LR, 1)
+            if s == 0:
+                prepare_weights()
+            if in_range(s - LQ - 1):
+                gains_and_store(s - LQ - 1)
             if in_range(s):
-                transpose_and_affine(s, 0)
-                regroup(nc.scalar.copy, s, 0)
-                transpose_and_affine(s, 1)
-            if in_range(s - 3):
-                multiply(s - 3)
+                transpose_and_affine(s, 0, "S")
+            if in_range(s + 1):
+                standard_deviation(s + 1)
+                reciprocal_std(s + 1)
+                if XS[s + 1]:
+                    make_shift(s + 1)
+                normalise(s + 1, "V")
+            if in_range(s):
+                if s < REGS:
+                    regroup(nc.scalar.copy, s, 0)
+                transpose_and_affine(s, 1, "V" if s >= AFFV else "S")
+            if in_range(s + 1):
+                normalise(s + 1, "S")
+            if in_range(s - LQ):
+                multiply(s - LQ)

@@ -21,13 +21,17 @@ COLS = HALVES * PACK
 RUN = 8
 EPS = 1e-6
 
-SIZES = [4] * 16
+SIZES = [2] + [4] * 15 + [2]
 GROUPS = len(SIZES)
 FIRST = [sum(SIZES[:g]) * P for g in range(GROUPS)]
-XG = [3] * 16
-XS = [1] + [0] * 15
+XG = [1,2] + [4] * 13 + [2, 0]
+XS = [1] + [0] * 16
 AFFV = GROUPS - 1
-REGS = GROUPS - 1
+LATE = [[]]+[[(1,3)]]*(GROUPS-1)
+SROWS = 512
+SREG = [256] + [SROWS] * 14 + [0, 0]
+HEAD = 2
+LPOS = 4
 LR = 1
 LQ = 2
 WQ = 1
@@ -53,37 +57,35 @@ def tile_realimagfourvallinear_pa_t_kernel(
         t_psum = ctx.enter_context(tc.psum_pool(name="t_psum", bufs=6))
         y_psum = ctx.enter_context(tc.psum_pool(name="y_psum", bufs=2))
 
-        affine_rows = const.tile([P, P], BF16)
+        affine_rows = const.tile([P, HALVES, P], BF16)
         nc.vector.memset(affine_rows[:], 0.0)
         for i, vec in enumerate((gamma, beta)):
-            for h in range(HALVES):
-                row = i * COLS + h * PACK
-                nc.scalar.dma_start(
-                    out=affine_rows[row : row + PACK, :].rearrange("t (b q) -> t b q", q=RUN),
-                    in_=vec[h * D : (h + 1) * D].rearrange("(b t q) -> t b q", t=PACK, q=RUN),
-                )
+            nc.scalar.dma_start(
+                out=affine_rows[i * PACK : (i + 1) * PACK].rearrange("t h c -> t (h c)").rearrange("t (hb q) -> t hb q", q=RUN),
+                in_=vec.rearrange("(hb t q) -> t hb q", t=PACK, q=RUN),
+            )
         w_sb = []
         for i, w in enumerate((qw_re, qw_im)):
             w_raw = const.tile([P, D], BF16, name="w_raw_%d" % i)
             nc.scalar.dma_start(out=w_raw[:], in_=w)
             w_sb.append(w_raw)
-        s_bf16 = []
-        for i, s in enumerate((s_re, s_im)):
-            s_sb = const.tile([P, 1], BF16, name="s_bf16_%d" % i)
-            nc.scalar.dma_start(out=s_sb[:], in_=s.partition_broadcast(P))
-            s_bf16.append(s_sb)
+        s_bf16 = [const.tile([P, 1], BF16, name="s_bf16_%d" % i) for i in range(2)]
+        one = const.tile([P, 1], F32)
+        nc.vector.memset(one[:], 1.0)
+        warm = const.tile([P, 1], F32)
+        nc.scalar.activation(out=warm[:], in_=one[:], func=ACT.Sqrt)
 
         ident_f32 = const.tile([P, P], F32)
         make_identity(nc, ident_f32[:])
         ident_bf16 = const.tile([P, P], BF16)
         gain_cols = const.tile([P, HALVES], F32)
-        affine_cols = const.tile([P, 2 * COLS], F32)
+        affine_cols = const.tile([P, HALVES, 2, PACK], F32)
         w_codes = const.tile([P, HALVES * 2 * N_OUT], U32, align_bytes=64)
         w_scales = const.tile([P, HALVES * 2 * N_OUT], U8, align_bytes=64)
         w_grouped = const.tile([P, HALVES * 2, N_OUT, PACK], BF16, align_bytes=64)
 
-        x_tiles, mean_var, std, neg_mean, rstd, shift, x_hat, planes, grouped, codes, scales, y_ps = (
-            {} for i in range(12)
+        x_tiles, mean_var, std, neg_mean, rstd, shift, x_hat_ts, x_hat, planes, grouped, codes, scales, y_ps = (
+            {} for i in range(13)
         )
 
         def load(g):
@@ -93,12 +95,14 @@ def tile_realimagfourvallinear_pa_t_kernel(
 
         def prepare_constants():
             nc.scalar.copy(out=ident_bf16[:], in_=ident_f32[:])
-            affine_ps = y_psum.tile([P, P], BF16, name="y_bank")
-            nc.tensor.transpose(affine_ps[:], affine_rows[:], ident_bf16[:])
-            nc.scalar.copy(out=affine_cols[:], in_=affine_ps[:, 0 : 2 * COLS])
+            affine_ps = y_psum.tile([P, HALVES, P], BF16, name="y_bank")
+            for h in range(HALVES):
+                nc.tensor.transpose(affine_ps[:, h, :], affine_rows[:, h, :], ident_bf16[:])
+            nc.scalar.copy(out=affine_cols[:].rearrange("p h i t -> p h (i t)"), in_=affine_ps[:, :, 0 : 2 * PACK])
 
-        def prepare_weights():
-            w_t = []
+        w_t = []
+
+        def transpose_weights():
             w_ps = y_psum.tile([P, 2, PACK, N_OUT], BF16, name="y_bank")
             for i in range(2):
                 w_runs = const.tile([P, PACK, P], BF16, name="w_runs_%d" % i)
@@ -109,6 +113,8 @@ def tile_realimagfourvallinear_pa_t_kernel(
                 for t in range(PACK):
                     nc.tensor.transpose(w_ps[:, i, t, :], w_runs[:, t, :], ident_bf16[:])
                 w_t.append(w_ps[:, i].rearrange("p t n -> p n t"))
+
+        def prepare_weights():
             nc.scalar.copy(out=w_grouped[:, 0], in_=w_t[0])
             nc.scalar.copy(out=w_grouped[:, 3], in_=w_t[0])
             nc.scalar.copy(out=w_grouped[:, 1], in_=w_t[1])
@@ -123,13 +129,15 @@ def tile_realimagfourvallinear_pa_t_kernel(
                 in_=w_grouped[:].rearrange("p q n t -> p (q n t)"),
             )
 
-        def statistics(g):
+        def statistics(g, between=None):
             T = SIZES[g]
             stats = small.tile([P, T, HALVES, 6], F32)
             mean_var[g] = small.tile([P, T, 2], F32, name="mean_var")
             for h in range(HALVES):
                 for j in range(T):
                     nc.vector.bn_stats(out=stats[:, j, h, :], in_=x_tiles[g][:, j, h, :])
+                    if between and (h * T + j == (1 if g <= HEAD else min(LPOS, HALVES * T - 1))):
+                        between()
             for j in range(T):
                 nc.vector.bn_aggr(out=mean_var[g][:, j, :], in_=stats[:, j].rearrange("p h c -> p (h c)"))
 
@@ -168,33 +176,41 @@ def tile_realimagfourvallinear_pa_t_kernel(
                 out=shift[g][:], in0=mean_var[g][:, :, 0], scalar=-1.0, in1=rstd[g][:], op0=ALU.mult, op1=ALU.mult
             )
 
+        def affine_on_vector(g, h, t):
+            nc.vector.tensor_scalar(
+                out=planes[g, h][:, t, :], in0=x_hat_ts[g, h, t][:], scalar1=affine_cols[:, h, 0, t : t + 1],
+                scalar2=affine_cols[:, h, 1, t : t + 1], op0=ALU.mult, op1=ALU.add,
+            )
+
         def transpose_and_affine(g, h, engine):
             T = SIZES[g]
             planes[g, h] = deep.tile([P, PACK, T * P], BF16, name="planes_%d" % h)
             if h == 0:
                 grouped[g] = deeper.tile([P, HALVES, T * P, PACK], BF16, align_bytes=64, name="grouped")
             for t in range(PACK):
-                c = h * PACK + t
                 x_hat_t = t_psum.tile([P, T * P], F32)
                 for j in range(T):
                     nc.tensor.transpose(
                         x_hat_t[:, j * P : (j + 1) * P], x_hat[g][:, j, t, h * P : (h + 1) * P], ident_f32[:]
                     )
+                x_hat_ts[g, h, t] = x_hat_t
+                if engine == "S" and (h, t) in LATE[g]:
+                    continue
                 if engine == "S":
                     nc.scalar.activation(
                         out=planes[g, h][:, t, :], in_=x_hat_t[:], func=ACT.Identity,
-                        scale=affine_cols[:, c : c + 1], bias=affine_cols[:, COLS + c : COLS + c + 1],
+                        scale=affine_cols[:, h, 0, t : t + 1], bias=affine_cols[:, h, 1, t : t + 1],
                     )
                 else:
-                    nc.vector.tensor_scalar(
-                        out=planes[g, h][:, t, :], in0=x_hat_t[:], scalar1=affine_cols[:, c : c + 1],
-                        scalar2=affine_cols[:, COLS + c : COLS + c + 1], op0=ALU.mult, op1=ALU.add,
-                    )
+                    affine_on_vector(g, h, t)
 
-        def regroup(copy, g, h):
+        def regroup(copy, g, h, a, b):
+            if a == b:
+                return
+            rows = slice(a, b)
             copy(
-                out=grouped[g][:, h].rearrange("p (c i) t -> p c t i", i=4),
-                in_=planes[g, h][:].rearrange("p t (c i) -> p c t i", i=4),
+                out=grouped[g][:, h, rows].rearrange("p (c i) t -> p c t i", i=4),
+                in_=planes[g, h][:, :, rows].rearrange("p t (c i) -> p c t i", i=4),
             )
 
         def quantise(g):
@@ -234,48 +250,66 @@ def tile_realimagfourvallinear_pa_t_kernel(
         def in_range(g):
             return 0 <= g < GROUPS
 
+        def begin(g):
+            reciprocal_std(g)
+            if XS[g]:
+                make_shift(g)
+            normalise(g, "V")
+
+        def begin_and_release(g):
+            begin(g)
+            release_normalise(g)
+
         for g in range(GROUPS):
             load(g)
+            if g == 3:
+                for i, s in enumerate((s_re, s_im)):
+                    nc.sync.dma_start(out=s_bf16[i][:], in_=s.partition_broadcast(P))
         statistics(0)
         prepare_constants()
+        transpose_weights()
         standard_deviation(0)
-        reciprocal_std(0)
-        if XS[0]:
-            make_shift(0)
-        normalise(0, "S")
-        normalise(0, "V")
+        if HEAD == 0:
+            begin(0)
 
         for s in range(GROUPS + LQ + 1):
-            if in_range(s):
-                release_normalise(s)
+            if s < HEAD:
+                statistics(s + 1, lambda: begin_and_release(s))
                 normalise(s, "G")
-            if in_range(s + 1):
-                statistics(s + 1)
-            if s == WQ:
-                quantise_weights()
-            if in_range(s - LQ):
-                quantise(s - LQ)
-            if in_range(s - LR):
-                if s - LR >= REGS:
-                    regroup(nc.vector.tensor_copy, s - LR, 0)
-                regroup(nc.vector.tensor_copy, s - LR, 1)
+                normalise(s, "S")
+                if s == 1 and LATE[0]:
+                    for h, t in LATE[0]:
+                        affine_on_vector(0, h, t)
+
+            def late():
+                if in_range(s - 1) and s - 1 < AFFV:
+                    for h, t in LATE[s - 1]:
+                        affine_on_vector(s - 1, h, t)
+
+            if in_range(s + 1) and s >= HEAD:
+                statistics(s + 1, late)
+            elif s >= HEAD:
+                late()
             if s == 0:
                 prepare_weights()
             if in_range(s - LQ - 1):
                 gains_and_store(s - LQ - 1)
-            if in_range(s):
-                transpose_and_affine(s, 0, "S")
             if in_range(s + 1):
                 standard_deviation(s + 1)
-                reciprocal_std(s + 1)
-                if XS[s + 1]:
-                    make_shift(s + 1)
-                normalise(s + 1, "V")
-            if in_range(s):
-                if s < REGS:
-                    regroup(nc.scalar.copy, s, 0)
-                transpose_and_affine(s, 1, "V" if s >= AFFV else "S")
-            if in_range(s + 1):
+            if s == WQ:
+                quantise_weights()
+            if in_range(s - LQ):
+                quantise(s - LQ)
+            if in_range(s + 1) and s + 1 >= HEAD:
+                begin_and_release(s + 1)
+                normalise(s + 1, "G")
                 normalise(s + 1, "S")
+            if in_range(s - LR):
+                regroup(nc.vector.tensor_copy, s - LR, 0, SREG[s - LR], SIZES[s - LR] * P)
+                regroup(nc.vector.tensor_copy, s - LR, 1, 0, SIZES[s - LR] * P)
+            if in_range(s):
+                transpose_and_affine(s, 0, "S")
+                regroup(nc.scalar.copy, s, 0, 0, SREG[s])
+                transpose_and_affine(s, 1, "V" if s >= AFFV else "S")
             if in_range(s - LQ):
                 multiply(s - LQ)

@@ -24,13 +24,15 @@ EPS = 1e-6
 SIZES = [2] + [4] * 15 + [2]
 GROUPS = len(SIZES)
 FIRST = [sum(SIZES[:g]) * P for g in range(GROUPS)]
-XG = [1,2] + [4] * 13 + [2, 0]
+XG = [1,3] + [4] * 13 + [2,0]
 XS = [1] + [0] * 16
 AFFV = GROUPS - 1
 LATE = [[]]+[[(1,3)]]*(GROUPS-1)
 SROWS = 512
 SREG = [256] + [SROWS] * 14 + [0, 0]
-HEAD = 2
+WT = 0
+PW = 1
+VX1 = 0
 LPOS = 4
 LR = 1
 LQ = 2
@@ -73,7 +75,7 @@ def tile_realimagfourvallinear_pa_t_kernel(
         one = const.tile([P, 1], F32)
         nc.vector.memset(one[:], 1.0)
         warm = const.tile([P, 1], F32)
-        nc.scalar.activation(out=warm[:], in_=one[:], func=ACT.Sqrt)
+        nc.scalar.activation(out=warm[:], in_=one[:], func=ACT.Abs_reciprocal_sqrt)
 
         ident_f32 = const.tile([P, P], F32)
         make_identity(nc, ident_f32[:])
@@ -84,8 +86,8 @@ def tile_realimagfourvallinear_pa_t_kernel(
         w_scales = const.tile([P, HALVES * 2 * N_OUT], U8, align_bytes=64)
         w_grouped = const.tile([P, HALVES * 2, N_OUT, PACK], BF16, align_bytes=64)
 
-        x_tiles, mean_var, std, neg_mean, rstd, shift, x_hat_ts, x_hat, planes, grouped, codes, scales, y_ps = (
-            {} for i in range(13)
+        x_tiles, mean_var, neg_mean, rstd, shift, x_hat_ts, x_hat, planes, grouped, codes, scales, y_ps = (
+            {} for i in range(12)
         )
 
         def load(g):
@@ -136,22 +138,22 @@ def tile_realimagfourvallinear_pa_t_kernel(
             for h in range(HALVES):
                 for j in range(T):
                     nc.vector.bn_stats(out=stats[:, j, h, :], in_=x_tiles[g][:, j, h, :])
-                    if between and (h * T + j == (1 if g <= HEAD else min(LPOS, HALVES * T - 1))):
+                    if between and (h * T + j == min(VX1 if g == 2 else LPOS, HALVES * T - 1)):
                         between()
             for j in range(T):
                 nc.vector.bn_aggr(out=mean_var[g][:, j, :], in_=stats[:, j].rearrange("p h c -> p (h c)"))
 
-        def standard_deviation(g):
-            std[g] = small.tile([P, SIZES[g]], F32, name="std")
-            nc.scalar.activation(out=std[g][:], in_=mean_var[g][:, :, 1], func=ACT.Sqrt, bias=EPS)
-
-        def reciprocal_std(g):
+        def scale_and_shift(g):
             rstd[g] = small.tile([P, SIZES[g]], F32, name="rstd")
-            nc.vector.reciprocal(out=rstd[g][:], in_=std[g][:])
-
-        def release_normalise(g):
+            nc.scalar.activation(out=rstd[g][:], in_=mean_var[g][:, :, 1], func=ACT.Abs_reciprocal_sqrt, bias=EPS)
             neg_mean[g] = small.tile([P, SIZES[g]], F32, name="neg_mean")
-            nc.vector.tensor_scalar_mul(out=neg_mean[g][:], in0=mean_var[g][:, :, 0], scalar1=-1.0)
+            nc.scalar.activation(out=neg_mean[g][:], in_=mean_var[g][:, :, 0], func=ACT.Copy, scale=-1.0)
+            if XS[g]:
+                shift[g] = small.tile([P, SIZES[g]], F32, name="shift")
+                for j in range(XG[g], XG[g] + XS[g]):
+                    nc.scalar.activation(
+                        out=shift[g][:, j : j + 1], in_=neg_mean[g][:, j : j + 1], func=ACT.Copy, scale=rstd[g][:, j : j + 1]
+                    )
 
         def normalise(g, kind):
             T = SIZES[g]
@@ -169,12 +171,6 @@ def tile_realimagfourvallinear_pa_t_kernel(
                     nc.vector.tensor_scalar(out=out, in0=x, scalar1=mean_var[g][:, j, 0:1], scalar2=r, op0=ALU.subtract, op1=ALU.mult)
                 else:
                     nc.scalar.activation(out=out, in_=x, func=ACT.Identity, scale=r, bias=shift[g][:, j : j + 1])
-
-        def make_shift(g):
-            shift[g] = small.tile([P, SIZES[g]], F32, name="shift")
-            nc.vector.scalar_tensor_tensor(
-                out=shift[g][:], in0=mean_var[g][:, :, 0], scalar=-1.0, in1=rstd[g][:], op0=ALU.mult, op1=ALU.mult
-            )
 
         def affine_on_vector(g, h, t):
             nc.vector.tensor_scalar(
@@ -250,16 +246,6 @@ def tile_realimagfourvallinear_pa_t_kernel(
         def in_range(g):
             return 0 <= g < GROUPS
 
-        def begin(g):
-            reciprocal_std(g)
-            if XS[g]:
-                make_shift(g)
-            normalise(g, "V")
-
-        def begin_and_release(g):
-            begin(g)
-            release_normalise(g)
-
         for g in range(GROUPS):
             load(g)
             if g == 3:
@@ -267,49 +253,52 @@ def tile_realimagfourvallinear_pa_t_kernel(
                     nc.sync.dma_start(out=s_bf16[i][:], in_=s.partition_broadcast(P))
         statistics(0)
         prepare_constants()
-        transpose_weights()
-        standard_deviation(0)
-        if HEAD == 0:
-            begin(0)
+        if WT == 0:
+            transpose_weights()
+        scale_and_shift(0)
+        normalise(0, "G")
+        normalise(0, "S")
+        if WT == 1:
+            transpose_weights()
 
         for s in range(GROUPS + LQ + 1):
-            if s < HEAD:
-                statistics(s + 1, lambda: begin_and_release(s))
-                normalise(s, "G")
-                normalise(s, "S")
-                if s == 1 and LATE[0]:
-                    for h, t in LATE[0]:
-                        affine_on_vector(0, h, t)
-
             def late():
+                if s == 0:
+                    normalise(0, "V")
+                if s == 1:
+                    normalise(1, "V")
                 if in_range(s - 1) and s - 1 < AFFV:
                     for h, t in LATE[s - 1]:
                         affine_on_vector(s - 1, h, t)
 
-            if in_range(s + 1) and s >= HEAD:
+            if in_range(s + 1):
                 statistics(s + 1, late)
-            elif s >= HEAD:
+            else:
                 late()
-            if s == 0:
+            if s == 0 and PW == 0:
                 prepare_weights()
             if in_range(s - LQ - 1):
                 gains_and_store(s - LQ - 1)
             if in_range(s + 1):
-                standard_deviation(s + 1)
+                scale_and_shift(s + 1)
+                normalise(s + 1, "G")
+                normalise(s + 1, "S")
+            if s == 0 and PW == 1:
+                prepare_weights()
             if s == WQ:
                 quantise_weights()
             if in_range(s - LQ):
                 quantise(s - LQ)
-            if in_range(s + 1) and s + 1 >= HEAD:
-                begin_and_release(s + 1)
-                normalise(s + 1, "G")
-                normalise(s + 1, "S")
             if in_range(s - LR):
                 regroup(nc.vector.tensor_copy, s - LR, 0, SREG[s - LR], SIZES[s - LR] * P)
                 regroup(nc.vector.tensor_copy, s - LR, 1, 0, SIZES[s - LR] * P)
+            if in_range(s + 1) and s >= 1:
+                normalise(s + 1, "V")
             if in_range(s):
                 transpose_and_affine(s, 0, "S")
                 regroup(nc.scalar.copy, s, 0, 0, SREG[s])
                 transpose_and_affine(s, 1, "V" if s >= AFFV else "S")
+            if s == 0 and PW == 2:
+                prepare_weights()
             if in_range(s - LQ):
                 multiply(s - LQ)

@@ -31,12 +31,12 @@ LATE = [[]]+[[(1,3)]]*(GROUPS-1)
 SROWS = 512
 SREG = [256] + [SROWS] * 14 + [0, 0]
 WT = 0
-PW = 1
+PW = 2
 VX1 = 0
 LPOS = 4
 LR = 1
 LQ = 2
-WQ = 1
+WQ = 2
 
 FLOPS = 4 * 2 * ROWS * D * N_OUT
 
@@ -143,11 +143,18 @@ def tile_realimagfourvallinear_pa_t_kernel(
             for j in range(T):
                 nc.vector.bn_aggr(out=mean_var[g][:, j, :], in_=stats[:, j].rearrange("p h c -> p (h c)"))
 
+        def minus_mean(g):
+            neg_mean[g] = small.tile([P, SIZES[g]], F32, name="neg_mean")
+            if g <= 1:
+                nc.scalar.activation(out=neg_mean[g][:], in_=mean_var[g][:, :, 0], func=ACT.Copy, scale=-1.0)
+            else:
+                nc.vector.tensor_scalar_mul(out=neg_mean[g][:], in0=mean_var[g][:, :, 0], scalar1=-1.0)
+
         def scale_and_shift(g):
             rstd[g] = small.tile([P, SIZES[g]], F32, name="rstd")
             nc.scalar.activation(out=rstd[g][:], in_=mean_var[g][:, :, 1], func=ACT.Abs_reciprocal_sqrt, bias=EPS)
-            neg_mean[g] = small.tile([P, SIZES[g]], F32, name="neg_mean")
-            nc.scalar.activation(out=neg_mean[g][:], in_=mean_var[g][:, :, 0], func=ACT.Copy, scale=-1.0)
+            if g <= 1:
+                minus_mean(g)
             if XS[g]:
                 shift[g] = small.tile([P, SIZES[g]], F32, name="shift")
                 for j in range(XG[g], XG[g] + XS[g]):
@@ -178,12 +185,13 @@ def tile_realimagfourvallinear_pa_t_kernel(
                 scalar2=affine_cols[:, h, 1, t : t + 1], op0=ALU.mult, op1=ALU.add,
             )
 
-        def transpose_and_affine(g, h, engine):
+        def transpose_and_affine(g, h, engine, ts):
             T = SIZES[g]
-            planes[g, h] = deep.tile([P, PACK, T * P], BF16, name="planes_%d" % h)
-            if h == 0:
+            if ts[0] == 0:
+                planes[g, h] = deep.tile([P, PACK, T * P], BF16, name="planes_%d" % h)
+            if h == 0 and ts[0] == 0:
                 grouped[g] = deeper.tile([P, HALVES, T * P, PACK], BF16, align_bytes=64, name="grouped")
-            for t in range(PACK):
+            for t in ts:
                 x_hat_t = t_psum.tile([P, T * P], F32)
                 for j in range(T):
                     nc.tensor.transpose(
@@ -281,7 +289,8 @@ def tile_realimagfourvallinear_pa_t_kernel(
                 gains_and_store(s - LQ - 1)
             if in_range(s + 1):
                 scale_and_shift(s + 1)
-                normalise(s + 1, "G")
+                if s == 0:
+                    normalise(s + 1, "G")
                 normalise(s + 1, "S")
             if s == 0 and PW == 1:
                 prepare_weights()
@@ -289,15 +298,19 @@ def tile_realimagfourvallinear_pa_t_kernel(
                 quantise_weights()
             if in_range(s - LQ):
                 quantise(s - LQ)
+            if s > 0 and in_range(s + 1):
+                minus_mean(s + 1)
+                normalise(s + 1, "G")
             if in_range(s - LR):
                 regroup(nc.vector.tensor_copy, s - LR, 0, SREG[s - LR], SIZES[s - LR] * P)
                 regroup(nc.vector.tensor_copy, s - LR, 1, 0, SIZES[s - LR] * P)
             if in_range(s + 1) and s >= 1:
                 normalise(s + 1, "V")
             if in_range(s):
-                transpose_and_affine(s, 0, "S")
+                transpose_and_affine(s, 0, "S", [0, 1, 2, 3])
+                transpose_and_affine(s, 1, "V" if s >= AFFV else "S", [0])
                 regroup(nc.scalar.copy, s, 0, 0, SREG[s])
-                transpose_and_affine(s, 1, "V" if s >= AFFV else "S")
+                transpose_and_affine(s, 1, "V" if s >= AFFV else "S", [1, 2, 3])
             if s == 0 and PW == 2:
                 prepare_weights()
             if in_range(s - LQ):

@@ -26,7 +26,7 @@ GROUPS = len(SIZES)
 FIRST = [sum(SIZES[:g]) * P for g in range(GROUPS)]
 XG = [1,3] + [4] * 13 + [2,0]
 XS = [1] + [0] * 16
-AFFV = GROUPS - 1
+AFFV = GROUPS
 LATE = [[]]+[[(1,3)]]*(GROUPS-1)
 SROWS = 512
 SREG = [256] + [SROWS] * 14 + [0, 0]
@@ -93,7 +93,12 @@ def tile_realimagfourvallinear_pa_t_kernel(
         def load(g):
             x_tiles[g] = x_pool.tile([P, SIZES[g], HALVES, D], BF16, name="x_sb")
             for h in range(HALVES):
-                nc.sync.dma_start(out=x_tiles[g][:, :, h, :], in_=rows_of((x_real, x_imag)[h], g))
+                x = rows_of((x_real, x_imag)[h], g)
+                if g == 0:
+                    for j in range(SIZES[g]):
+                        nc.sync.dma_start(out=x_tiles[g][:, j, h, :], in_=x[:, j, :])
+                else:
+                    nc.sync.dma_start(out=x_tiles[g][:, :, h, :], in_=x)
 
         def prepare_constants():
             nc.scalar.copy(out=ident_bf16[:], in_=ident_f32[:])

from contextlib import ExitStack

import concourse.mybir as mybir
from concourse.masks import make_identity

F32 = mybir.dt.float32
BF16 = mybir.dt.bfloat16
U32 = mybir.dt.uint32
U8 = mybir.dt.uint8
FP8X4 = mybir.dt.float8_e4m3fn_x4
ACT = mybir.ActivationFunctionType
ALU = mybir.AluOpType

P = 128
PACK = 4
ROWS = 4 * 2048
D = 512
N_OUT = 128
HALVES = 2
COLS = HALVES * PACK
RUN = 8
EPS = 1e-6

SIZES = [2] + [4] * 15 + [2]
GROUPS = len(SIZES)
FIRST = [sum(SIZES[:g]) * P for g in range(GROUPS)]
XG = [1,3] + [4] * 13 + [2,0]
XS = [1] + [0] * 16
AFFV = GROUPS
LATE = [[]]+[[(1,3)]]*(GROUPS-1)
SROWS = 512
SREG = [256] + [SROWS] * 14 + [0, 0]
WT = 0
PW = 2
VX1 = 0
LPOS = 4
LR = 1
LQ = 2
WQ = 2

FLOPS = 4 * 2 * ROWS * D * N_OUT


def tile_realimagfourvallinear_pa_t_kernel(
    tc, x_real, x_imag, qw_re, qw_im, gamma, beta, s_re, s_im, out_0, out_1
):
    nc = tc.nc
    def rows_of(dram, g):
        return dram.flatten_outer_dims()[FIRST[g] : FIRST[g] + SIZES[g] * P].rearrange("(p j) k -> p j k", j=SIZES[g])

    with ExitStack() as ctx:
        ctx.enter_context(tc.manual_schedule())
        const = ctx.enter_context(tc.tile_pool(name="const", bufs=1))
        x_pool = ctx.enter_context(tc.tile_pool(name="x_pool", bufs=12))
        small = ctx.enter_context(tc.tile_pool(name="small", bufs=4))
        work = ctx.enter_context(tc.tile_pool(name="work", bufs=2))
        deep = ctx.enter_context(tc.tile_pool(name="deep", bufs=3))
        deeper = ctx.enter_context(tc.tile_pool(name="deeper", bufs=4))
        t_psum = ctx.enter_context(tc.psum_pool(name="t_psum", bufs=6))
        y_psum = ctx.enter_context(tc.psum_pool(name="y_psum", bufs=2))

        affine_rows = const.tile([P, HALVES, P], BF16)
        nc.vector.memset(affine_rows[:], 0.0)
        for i, vec in enumerate((gamma, beta)):
            nc.scalar.dma_start(
                out=affine_rows[i * PACK : (i + 1) * PACK].rearrange("t h c -> t (h c)").rearrange("t (hb q) -> t hb q", q=RUN),
                in_=vec.rearrange("(hb t q) -> t hb q", t=PACK, q=RUN),
            )
        w_sb = []
        for i, w in enumerate((qw_re, qw_im)):
            w_raw = const.tile([P, D], BF16, name="w_raw_%d" % i)
            nc.scalar.dma_start(out=w_raw[:], in_=w)
            w_sb.append(w_raw)
        s_bf16 = [const.tile([P, 1], BF16, name="s_bf16_%d" % i) for i in range(2)]
        one = const.tile([P, 1], F32)
        nc.vector.memset(one[:], 1.0)
        warm = const.tile([P, 1], F32)
        nc.scalar.activation(out=warm[:], in_=one[:], func=ACT.Abs_reciprocal_sqrt)

        ident_f32 = const.tile([P, P], F32)
        make_identity(nc, ident_f32[:])
        ident_bf16 = const.tile([P, P], BF16)
        gain_cols = const.tile([P, HALVES], F32)
        affine_cols = const.tile([P, HALVES, 2, PACK], F32)
        w_codes = const.tile([P, HALVES * 2 * N_OUT], U32, align_bytes=64)
        w_scales = const.tile([P, HALVES * 2 * N_OUT], U8, align_bytes=64)
        w_grouped = const.tile([P, HALVES * 2, N_OUT, PACK], BF16, align_bytes=64)

        x_tiles, mean_var, neg_mean, rstd, shift, x_hat_ts, x_hat, planes, grouped, codes, scales, y_ps = (
            {} for i in range(12)
        )

        def load(g):
            x_tiles[g] = x_pool.tile([P, SIZES[g], HALVES, D], BF16, name="x_sb")
            for h in range(HALVES):
                x = rows_of((x_real, x_imag)[h], g)
                if g == 0:
                    for j in range(SIZES[g]):
                        nc.sync.dma_start(out=x_tiles[g][:, j, h, :], in_=x[:, j, :])
                else:
                    nc.sync.dma_start(out=x_tiles[g][:, :, h, :], in_=x)

        def prepare_constants():
            nc.scalar.copy(out=ident_bf16[:], in_=ident_f32[:])
            affine_ps = y_psum.tile([P, HALVES, P], BF16, name="y_bank")
            for h in range(HALVES):
                nc.tensor.transpose(affine_ps[:, h, :], affine_rows[:, h, :], ident_bf16[:])
            nc.scalar.copy(out=affine_cols[:].rearrange("p h i t -> p h (i t)"), in_=affine_ps[:, :, 0 : 2 * PACK])

        w_t = []

        def transpose_weights():
            w_ps = y_psum.tile([P, 2, PACK, N_OUT], BF16, name="y_bank")
            for i in range(2):
                w_runs = const.tile([P, PACK, P], BF16, name="w_runs_%d" % i)
                nc.scalar.copy(
                    out=w_runs[:].rearrange("n t (b q) -> n t b q", q=RUN),
                    in_=w_sb[i][:].rearrange("n (b t q) -> n t b q", t=PACK, q=RUN),
                )
                for t in range(PACK):
                    nc.tensor.transpose(w_ps[:, i, t, :], w_runs[:, t, :], ident_bf16[:])
                w_t.append(w_ps[:, i].rearrange("p t n -> p n t"))

        def prepare_weights():
            nc.scalar.copy(out=w_grouped[:, 0], in_=w_t[0])
            nc.scalar.copy(out=w_grouped[:, 3], in_=w_t[0])
            nc.scalar.copy(out=w_grouped[:, 1], in_=w_t[1])
            nc.scalar.activation(out=w_grouped[:, 2], in_=w_t[1], func=ACT.Copy, scale=-1.0)
            for i in range(2):
                nc.scalar.copy(out=gain_cols[:, i : i + 1], in_=s_bf16[i][:])

        def quantise_weights():
            nc.vector.quantize_mx(
                out=w_codes[:].bitcast(FP8X4),
                scales=w_scales[:],
                in_=w_grouped[:].rearrange("p q n t -> p (q n t)"),
            )

        def statistics(g, between=None):
            T = SIZES[g]
            stats = small.tile([P, T, HALVES, 6], F32)
            mean_var[g] = small.tile([P, T, 2], F32, name="mean_var")
            for h in range(HALVES):
                for j in range(T):
                    nc.vector.bn_stats(out=stats[:, j, h, :], in_=x_tiles[g][:, j, h, :])
                    if between and (h * T + j == min(VX1 if g == 2 else LPOS, HALVES * T - 1)):
                        between()
            for j in range(T):
                nc.vector.bn_aggr(out=mean_var[g][:, j, :], in_=stats[:, j].rearrange("p h c -> p (h c)"))

        def minus_mean(g):
            neg_mean[g] = small.tile([P, SIZES[g]], F32, name="neg_mean")
            if g <= 1:
                nc.scalar.activation(out=neg_mean[g][:], in_=mean_var[g][:, :, 0], func=ACT.Copy, scale=-1.0)
            else:
                nc.vector.tensor_scalar_mul(out=neg_mean[g][:], in0=mean_var[g][:, :, 0], scalar1=-1.0)

        def scale_and_shift(g):
            rstd[g] = small.tile([P, SIZES[g]], F32, name="rstd")
            nc.scalar.activation(out=rstd[g][:], in_=mean_var[g][:, :, 1], func=ACT.Abs_reciprocal_sqrt, bias=EPS)
            if g <= 1:
                minus_mean(g)
            if XS[g]:
                shift[g] = small.tile([P, SIZES[g]], F32, name="shift")
                for j in range(XG[g], XG[g] + XS[g]):
                    nc.scalar.activation(
                        out=shift[g][:, j : j + 1], in_=neg_mean[g][:, j : j + 1], func=ACT.Copy, scale=rstd[g][:, j : j + 1]
                    )

        def normalise(g, kind):
            T = SIZES[g]
            if g not in x_hat:
                x_hat[g] = work.tile([P, T, PACK, HALVES * P], F32, name="x_hat")
            a, b = XG[g], XG[g] + XS[g]
            tiles = {"G": range(a), "S": range(a, b), "V": range(b, T)}[kind]
            for j in tiles:
                out = x_hat[g][:, j].rearrange("p t (hb q) -> p t hb q", q=RUN)
                x = x_tiles[g][:, j].rearrange("p h k -> p (h k)").rearrange("p (hb t q) -> p t hb q", t=PACK, q=RUN)
                r = rstd[g][:, j : j + 1]
                if kind == "G":
                    nc.gpsimd.tensor_scalar(out=out, in0=x, scalar1=neg_mean[g][:, j : j + 1], scalar2=r, op0=ALU.add, op1=ALU.mult)
                elif kind == "V":
                    nc.vector.tensor_scalar(out=out, in0=x, scalar1=mean_var[g][:, j, 0:1], scalar2=r, op0=ALU.subtract, op1=ALU.mult)
                else:
                    nc.scalar.activation(out=out, in_=x, func=ACT.Identity, scale=r, bias=shift[g][:, j : j + 1])

        def affine_on_vector(g, h, t):
            nc.vector.tensor_scalar(
                out=planes[g, h][:, t, :], in0=x_hat_ts[g, h, t][:], scalar1=affine_cols[:, h, 0, t : t + 1],
                scalar2=affine_cols[:, h, 1, t : t + 1], op0=ALU.mult, op1=ALU.add,
            )

        def transpose_and_affine(g, h, engine, ts):
            T = SIZES[g]
            if ts[0] == 0:
                planes[g, h] = deep.tile([P, PACK, T * P], BF16, name="planes_%d" % h)
            if h == 0 and ts[0] == 0:
                grouped[g] = deeper.tile([P, HALVES, T * P, PACK], BF16, align_bytes=64, name="grouped")
            for t in ts:
                x_hat_t = t_psum.tile([P, T * P], F32)
                for j in range(T):
                    nc.tensor.transpose(
                        x_hat_t[:, j * P : (j + 1) * P], x_hat[g][:, j, t, h * P : (h + 1) * P], ident_f32[:]
                    )
                x_hat_ts[g, h, t] = x_hat_t
                if engine == "S" and (h, t) in LATE[g]:
                    continue
                if engine == "S":
                    nc.scalar.activation(
                        out=planes[g, h][:, t, :], in_=x_hat_t[:], func=ACT.Identity,
                        scale=affine_cols[:, h, 0, t : t + 1], bias=affine_cols[:, h, 1, t : t + 1],
                    )
                else:
                    affine_on_vector(g, h, t)

        def regroup(copy, g, h, a, b):
            if a == b:
                return
            rows = slice(a, b)
            copy(
                out=grouped[g][:, h, rows].rearrange("p (c i) t -> p c t i", i=4),
                in_=planes[g, h][:, :, rows].rearrange("p t (c i) -> p c t i", i=4),
            )

        def quantise(g):
            codes[g] = work.tile([P, HALVES, SIZES[g] * P], U32, align_bytes=64, name="codes")
            scales[g] = work.tile([P, HALVES, SIZES[g] * P], U8, align_bytes=64, name="scales")
            nc.vector.quantize_mx(
                out=codes[g][:].rearrange("p h r -> p (h r)").bitcast(FP8X4),
                scales=scales[g][:].rearrange("p h r -> p (h r)"),
                in_=grouped[g][:].rearrange("p h r t -> p (h r t)"),
            )

        def multiply(g):
            y_ps[g] = []
            for c in range(HALVES):
                y_bank = y_psum.tile([P, SIZES[g], N_OUT], F32, name="y_bank")
                for j in range(SIZES[g]):
                    rows = slice(j * P, (j + 1) * P)
                    for h in range(HALVES):
                        cols = slice((2 * h + c) * N_OUT, (2 * h + c + 1) * N_OUT)
                        nc.tensor.matmul_mx(
                            out=y_bank[:, j, :],
                            lhsT=codes[g][:, h, rows].bitcast(FP8X4),
                            lhsT_scale=scales[g][:, h, rows],
                            rhs=w_codes[:, cols].bitcast(FP8X4),
                            rhs_scale=w_scales[:, cols],
                            start=(h == 0),
                            stop=(h == HALVES - 1),
                        )
                y_ps[g].append(y_bank)

        def gains_and_store(g):
            for c in range(HALVES):
                y_sb = work.tile([P, SIZES[g], N_OUT], F32, name="y_sb_%d" % c)
                nc.scalar.activation(out=y_sb[:], in_=y_ps[g][c][:], func=ACT.Copy, scale=gain_cols[:, c : c + 1])
                nc.sync.dma_start(out=rows_of((out_0, out_1)[c], g), in_=y_sb[:])

        def in_range(g):
            return 0 <= g < GROUPS

        for g in range(GROUPS):
            load(g)
            if g == 3:
                for i, s in enumerate((s_re, s_im)):
                    nc.sync.dma_start(out=s_bf16[i][:], in_=s.partition_broadcast(P))
        statistics(0)
        prepare_constants()
        if WT == 0:
            transpose_weights()
        scale_and_shift(0)
        normalise(0, "G")
        normalise(0, "S")
        if WT == 1:
            transpose_weights()

        for s in range(GROUPS + LQ + 1):
            def late():
                if s == 0:
                    normalise(0, "V")
                if s == 1:
                    normalise(1, "V")
                if in_range(s - 1) and s - 1 < AFFV:
                    for h, t in LATE[s - 1]:
                        affine_on_vector(s - 1, h, t)

            if in_range(s + 1):
                statistics(s + 1, late)
            else:
                late()
            if s == 0 and PW == 0:
                prepare_weights()
            if in_range(s - LQ - 1):
                gains_and_store(s - LQ - 1)
            if in_range(s + 1):
                scale_and_shift(s + 1)
                if s == 0:
                    normalise(s + 1, "G")
                normalise(s + 1, "S")
            if s == 0 and PW == 1:
                prepare_weights()
            if s == WQ:
                quantise_weights()
            if in_range(s - LQ):
                quantise(s - LQ)
            if s > 0 and in_range(s + 1):
                minus_mean(s + 1)
                normalise(s + 1, "G")
            if in_range(s - LR):
                regroup(nc.vector.tensor_copy, s - LR, 0, SREG[s - LR], SIZES[s - LR] * P)
                regroup(nc.vector.tensor_copy, s - LR, 1, 0, SIZES[s - LR] * P)
            if in_range(s + 1) and s >= 1:
                normalise(s + 1, "V")
            if in_range(s):
                transpose_and_affine(s, 0, "S", [0, 1, 2, 3])
                transpose_and_affine(s, 1, "V" if s >= AFFV else "S", [0])
                regroup(nc.scalar.copy, s, 0, 0, SREG[s])
                transpose_and_affine(s, 1, "V" if s >= AFFV else "S", [1, 2, 3])
            if s == 0 and PW == 2:
                prepare_weights()
            if in_range(s - LQ):
                multiply(s - LQ)
